import numpy as np
import ml_dtypes


def mxq(x, axis, fmt="e4m3"):
    dtype, down = {"e4m3": (ml_dtypes.float8_e4m3fn, 7), "e5m2": (ml_dtypes.float8_e5m2, 14)}[fmt]
    v = np.moveaxis(np.asarray(x, np.float32).astype(ml_dtypes.bfloat16).astype(np.float64), axis, -1)
    blocks = v.reshape(v.shape[:-1] + (-1, 32))
    amax = np.abs(blocks).max(-1, keepdims=True)
    byte = np.maximum(np.where(amax > 0, np.frexp(amax)[1] - 1 + 127, 0) - down, 1)
    scale = np.exp2(byte - 127.0)
    codes = (blocks / scale).astype(np.float32).astype(dtype).astype(np.float64)
    return np.moveaxis((codes * scale).reshape(v.shape), -1, axis)


WIDE = False


def mx_kscale(k):
    if not WIDE:
        return np.ones(k)
    levels = np.array([10, -10, 5, -5, 0])
    a = np.random.permutation(np.resize(levels, k // 512 * 4)).reshape(k // 512, 4)
    idx = np.arange(k)
    return np.exp2(a[idx // 512, idx % 128 // 32])


BF16 = ml_dtypes.bfloat16


def bf(x):
    return np.asarray(x, np.float32).astype(BF16)


def f64(x):
    return np.asarray(x).astype(np.float64)


E2M1 = np.array([0.0, 0.5, 1.0, 1.5, 2.0, 3.0, 4.0, 6.0, -0.0, -0.5, -1.0, -1.5, -2.0, -3.0, -4.0, -6.0])


def pack_weight(w, fmt):
    k, n = w.shape
    w = f64(bf(w)).reshape(k // 32, 32, n)
    amax = np.abs(w).max(1)
    if fmt == "e4m3":
        byte = np.frexp(amax)[1] - 1 + 127 - 7
    else:
        mant, ex = np.frexp(amax / 6.0)
        byte = np.where(mant > 0.5, ex, ex - 1) + 127
    byte = np.clip(np.where(amax > 0, byte, 1), 1, 254)
    scaled = (w * np.exp2(127.0 - byte)[:, None, :]).reshape(k, n).astype(np.float32)
    by_word = np.ascontiguousarray(scaled.reshape(k // 512, 128, 4, n).transpose(0, 1, 3, 2))
    if fmt == "e4m3":
        words = by_word.astype(ml_dtypes.float8_e4m3fn).view(np.uint8)
    else:
        c = by_word.astype(ml_dtypes.float4_e2m1fn).view(np.uint8) & 0xF
        words = c[..., 0::2] | (c[..., 1::2] << 4)
    return np.ascontiguousarray(words), np.ascontiguousarray(byte.astype(np.uint8).reshape(k // 512, 16, n))


def unpack_weight(words, scales, fmt):
    g, p, n, _ = words.shape
    if fmt == "e4m3":
        vals = np.ascontiguousarray(words).view(ml_dtypes.float8_e4m3fn).astype(np.float64)
    else:
        nib = np.empty((g, p, n, 4), np.uint8)
        nib[..., 0::2] = words & 0xF
        nib[..., 1::2] = words >> 4
        vals = E2M1[nib]
    vals = vals * np.repeat(np.exp2(scales.astype(np.float64) - 127.0), 8, axis=1)[..., None]
    return vals.transpose(0, 1, 3, 2).reshape(g * 512, n)

def pack4(w):
    words, scales = pack_weight(w, "e2m1")
    return words.reshape(words.shape[0], 128, -1), scales


def unpack4(words, scales):
    return unpack_weight(words.reshape(words.shape[0], 128, -1, 2), scales, "e2m1")


B, H = 256, 512
K = 2 * H
BETA_SHIFT = 1.0
LN_EPS = 1e-5
BAG_EPS = 1e-6


def setup_inputs():
    s = mx_kscale(H)
    r_main = np.random.uniform(0.5, 1.1, (B, 1))
    r_branch = np.random.uniform(0.5, 1.1, (B, 1))
    w_mb = np.random.standard_normal((K, H)) / np.sqrt(K)
    w_mb[H:] = w_mb[H:] / s[:, None]
    main = bf(np.random.standard_normal((B, H)) * r_main)
    branch = bf(np.random.standard_normal((B, H)) * r_branch * s)
    o = bf(1.0 - np.random.random((B, 1)) * np.random.uniform(0.2, 0.8, (B, H)))
    is_bag = bf(np.random.random((B, 1)))
    W_mb_words, W_mb_scales = pack4(w_mb)
    b_mb = bf(np.random.standard_normal(H) * 0.3)
    W_b_words, W_b_scales = pack4(np.random.standard_normal((H, H)) * 2.0 / np.sqrt(H) / s[:, None])
    b_b = bf(np.random.standard_normal(H) * 0.3)
    ln_g = bf(1.0 + 0.1 * np.random.standard_normal(H))
    ln_b = bf(0.1 * np.random.standard_normal(H))
    return {"main": main,
            "branch": branch,
            "o": o,
            "is_bag": is_bag,
            "W_mb_words": W_mb_words,
            "W_mb_scales": W_mb_scales,
            "b_mb": b_mb,
            "W_b_words": W_b_words,
            "W_b_scales": W_b_scales,
            "b_b": b_b,
            "ln_g": ln_g,
            "ln_b": ln_b}


def reference(main, branch, o, is_bag, W_mb_words, W_mb_scales, b_mb, W_b_words, W_b_scales, b_b, ln_g, ln_b):
    main, is_bag = f64(main), f64(is_bag)
    mbq = mxq(np.concatenate([main, f64(branch)], axis=-1), 1, "e4m3")
    weight_b = np.maximum((mbq @ unpack4(W_mb_words, W_mb_scales)) + f64(b_mb), 0.0)
    h_m = weight_b * ((mbq[:, H:] @ unpack4(W_b_words, W_b_scales)) + f64(b_b))
    em_norm = np.sqrt((main ** 2).sum(-1))
    hm_norm = np.sqrt((h_m ** 2).sum(-1))
    hm_norm = np.where(hm_norm == 0, np.ones_like(hm_norm), hm_norm)
    alpha = np.minimum(em_norm / (hm_norm + BAG_EPS) * BETA_SHIFT, 1.0)[:, None]
    pre = alpha * h_m + main
    mu = pre.mean(-1, keepdims=True)
    var = ((pre - mu) ** 2).mean(-1, keepdims=True)
    emb = (pre - mu) / np.sqrt(var + LN_EPS) * f64(ln_g) + f64(ln_b)
    shift_c = emb * is_bag + main * (1.0 - is_bag)
    h = f64(o) * np.tanh(shift_c)
    return h, shift_c

@@ -1,0 +1,239 @@
+from contextlib import ExitStack
+
+import concourse.mybir as mybir
+from concourse.masks import make_identity
+
+FP8X4 = mybir.dt.float8_e4m3fn_x4
+FP4X4 = mybir.dt.float4_e2m1fn_x4
+BF16 = mybir.dt.bfloat16
+F32 = mybir.dt.float32
+I32 = mybir.dt.int32
+U32 = mybir.dt.uint32
+U8 = mybir.dt.uint8
+ALU = mybir.AluOpType
+ACT = mybir.ActivationFunctionType
+
+P = 128
+B = 256
+H = 512
+ROW_TILES = B // P
+WORDS = H // 2
+LN_EPS = 1e-5
+BAG_EPS = 1e-6
+
+FLOPS = 2 * B * (2 * H) * H + 2 * B * H * H
+
+
+def tile_bag_lstm_pb_s_kernel(
+    tc,
+    main,
+    branch,
+    o,
+    is_bag,
+    W_mb_words,
+    W_mb_scales,
+    b_mb,
+    W_b_words,
+    W_b_scales,
+    b_b,
+    ln_g,
+    ln_b,
+    out_0,
+    out_1,
+):
+    nc = tc.nc
+
+    def by_row_tile(ap):
+        return ap.rearrange("(p t) c -> p t c", t=ROW_TILES)
+
+    with ExitStack() as ctx:
+        keep = ctx.enter_context(tc.tile_pool(name="keep", bufs=1))
+        psum = ctx.enter_context(tc.psum_pool(name="psum", bufs=1))
+
+        w_scales = keep.tile([P, 3, H], U8, align_bytes=64)
+        nc.vector.memset(w_scales[:].rearrange("p g n -> p (g n)").bitcast(I32), 0)
+        warm = keep.tile([P, 1], F32)
+        nc.vector.memset(warm[:], 0.0)
+        nc.scalar.activation(out=warm[:], in_=warm[:], func=ACT.Tanh)
+        ident = keep.tile([P, P], F32)
+        make_identity(nc, ident[:])
+        half = keep.tile([P, ROW_TILES], F32)
+        nc.gpsimd.memset(half[:], 0.5)
+        neg_half = keep.tile([P, 1], F32)
+        nc.gpsimd.memset(neg_half[:], -0.5)
+
+        main_sb = keep.tile([P, ROW_TILES, H], BF16)
+        nc.sync.dma_start(out=main_sb[:], in_=by_row_tile(main))
+        branch_sb = keep.tile([P, ROW_TILES, H], BF16)
+        nc.sync.dma_start(out=branch_sb[:], in_=by_row_tile(branch))
+        w_words = keep.tile([P, 3, 2 * H], U8, align_bytes=64)
+        nc.sync.dma_start(
+            out=w_words[:, 0:2, :].bitcast(I32),
+            in_=W_mb_words.rearrange("g p n -> p g n").bitcast(I32),
+        )
+        for r in range(4):
+            nc.sync.dma_start(
+                out=w_scales[r:P:32, 0:2, :].bitcast(I32),
+                in_=W_mb_scales[:, r:16:4, :].rearrange("g q n -> q g n").bitcast(I32),
+            )
+        nc.sync.dma_start(out=w_words[:, 2, :].bitcast(I32), in_=W_b_words[0].bitcast(I32))
+        for r in range(4):
+            nc.sync.dma_start(
+                out=w_scales[r:P:32, 2, :].bitcast(I32),
+                in_=W_b_scales[0, r:16:4, :].bitcast(I32),
+            )
+        o_sb = keep.tile([P, ROW_TILES, H], BF16)
+        nc.sync.dma_start(out=o_sb[:], in_=by_row_tile(o))
+
+        bag_bf = keep.tile([P, ROW_TILES], BF16)
+        nc.gpsimd.dma_start(out=bag_bf[:], in_=is_bag.rearrange("(p t) one -> p (t one)", t=ROW_TILES))
+        ln_b_all = keep.tile([P, H], BF16)
+        nc.gpsimd.dma_start(out=ln_b_all[:], in_=ln_b.partition_broadcast(P))
+        b_mb_all = keep.tile([P, H], BF16)
+        nc.gpsimd.dma_start(out=b_mb_all[:], in_=b_mb.partition_broadcast(P))
+        b_b_all = keep.tile([P, H], BF16)
+        nc.gpsimd.dma_start(out=b_b_all[:], in_=b_b.partition_broadcast(P))
+        ln_g_all = keep.tile([P, H], BF16)
+        nc.gpsimd.dma_start(out=ln_g_all[:], in_=ln_g.partition_broadcast(P))
+
+        x_codes = keep.tile([P, 2, B], U32, align_bytes=64)
+        x_scales = keep.tile([P, 2, B], U8, align_bytes=64)
+        grouped = []
+        for g, x_sb in enumerate((main_sb, branch_sb)):
+            flipped = psum.tile([P, 2, B], F32, name="flipped%d" % g)
+            for t in range(ROW_TILES):
+                words = x_sb[:, t, :].bitcast(F32)
+                for u in range(2):
+                    nc.tensor.transpose(flipped[:, u, t * P : (t + 1) * P], words[:, u:WORDS:2], ident[:])
+            side_by_side = keep.tile([P, 4 * B], BF16, align_bytes=64, name="grouped%d" % g)
+            dst = side_by_side[:].bitcast(F32).rearrange("p (c u) -> p c u", u=2)
+            src = flipped[:].rearrange("p u c -> p c u")
+            if g == 0:
+                nc.vector.tensor_copy(out=dst, in_=src)
+            else:
+                nc.scalar.copy(out=dst, in_=src)
+            grouped.append(side_by_side)
+        for g in range(2):
+            nc.vector.quantize_mx(
+                out=x_codes[:, g, :].bitcast(FP8X4), scales=x_scales[:, g, :], in_=grouped[g][:]
+            )
+
+        def mx_pass(acc, t, g, w, start, stop):
+            rows = slice(t * P, (t + 1) * P)
+            nc.tensor.matmul_mx(
+                out=acc[:],
+                lhsT=x_codes[:, g, rows].bitcast(FP8X4),
+                lhsT_scale=x_scales[:, g, rows],
+                rhs=w_words[:, w, :].bitcast(FP4X4),
+                rhs_scale=w_scales[:, w, :],
+                start=start,
+                stop=stop,
+            )
+
+        gate_acc = []
+        lin_acc = []
+        for t in range(ROW_TILES):
+            gate = psum.tile([P, H], F32, name="gate_acc%d" % t)
+            mx_pass(gate, t, 0, 0, True, False)
+            mx_pass(gate, t, 1, 1, False, True)
+            lin = psum.tile([P, H], F32, name="lin_acc%d" % t)
+            mx_pass(lin, t, 1, 2, True, True)
+            gate_acc.append(gate)
+            lin_acc.append(lin)
+
+        bag = keep.tile([P, ROW_TILES], F32)
+        nc.vector.tensor_copy(out=bag[:], in_=bag_bf[:])
+        one_minus_bag = keep.tile([P, ROW_TILES], F32)
+        nc.vector.tensor_scalar(
+            out=one_minus_bag[:], in0=bag[:], scalar1=-1.0, scalar2=1.0, op0=ALU.mult, op1=ALU.add
+        )
+        squares = keep.tile([P, H], F32)
+        em_sq = keep.tile([P, ROW_TILES], F32)
+        gain = []
+        rest = []
+        for t in range(ROW_TILES):
+            col = slice(t, t + 1)
+            nc.scalar.activation(
+                out=squares[:], in_=main_sb[:, t, :], func=ACT.Square, accum_out=em_sq[:, col]
+            )
+            kept = keep.tile([P, H], F32, name="kept%d" % t)
+            nc.scalar.activation(out=kept[:], in_=main_sb[:, t, :], func=ACT.Copy, scale=one_minus_bag[:, col])
+            rest_t = keep.tile([P, H], F32, name="rest%d" % t)
+            nc.vector.scalar_tensor_tensor(
+                out=rest_t[:], in0=ln_b_all[:], scalar=bag[:, col], in1=kept[:], op0=ALU.mult, op1=ALU.add
+            )
+            gain_t = keep.tile([P, H], F32, name="gain%d" % t)
+            nc.scalar.activation(out=gain_t[:], in_=ln_g_all[:], func=ACT.Copy, scale=bag[:, col])
+            gain.append(gain_t)
+            rest.append(rest_t)
+        em = keep.tile([P, ROW_TILES], F32)
+        nc.gpsimd.tensor_tensor(out=em[:], in0=em_sq[:], in1=half[:], op=ALU.pow)
+
+        for t in range(ROW_TILES):
+            col = slice(t, t + 1)
+
+            def big(name):
+                return keep.tile([P, H], F32, name="%s%d" % (name, t))
+
+            def small(name):
+                return keep.tile([P, 1], F32, name="%s%d" % (name, t))
+
+            gate_b = big("gate_b")
+            nc.vector.tensor_tensor(out=gate_b[:], in0=gate_acc[t][:], in1=b_mb_all[:], op=ALU.add)
+            lin_b = big("lin_b")
+            nc.vector.tensor_tensor(out=lin_b[:], in0=lin_acc[t][:], in1=b_b_all[:], op=ALU.add)
+            h_m = big("h_m")
+            nc.vector.scalar_tensor_tensor(
+                out=h_m[:], in0=gate_b[:], scalar=0.0, in1=lin_b[:], op0=ALU.max, op1=ALU.mult
+            )
+
+            hm_sq = small("hm_sq")
+            nc.scalar.activation(out=squares[:], in_=h_m[:], func=ACT.Square, accum_out=hm_sq[:])
+            hm = small("hm")
+            nc.gpsimd.tensor_tensor(out=hm[:], in0=hm_sq[:], in1=half[:, 0:1], op=ALU.pow)
+            alpha = small("alpha")
+            nc.vector.tensor_scalar_add(out=alpha[:], in0=hm[:], scalar1=BAG_EPS)
+            nc.vector.reciprocal(out=alpha[:], in_=alpha[:])
+            nc.vector.tensor_scalar(
+                out=alpha[:], in0=alpha[:], scalar1=em[:, col], scalar2=1.0, op0=ALU.mult, op1=ALU.min
+            )
+
+            pre = big("pre")
+            pre_sum = small("pre_sum")
+            nc.vector.scalar_tensor_tensor(
+                out=pre[:],
+                in0=h_m[:],
+                scalar=alpha[:],
+                in1=main_sb[:, t, :],
+                op0=ALU.mult,
+                op1=ALU.add,
+                accum_out=pre_sum[:],
+            )
+            neg_mu = small("neg_mu")
+            nc.vector.tensor_scalar_mul(out=neg_mu[:], in0=pre_sum[:], scalar1=-1.0 / H)
+
+            dev_sq = small("dev_sq")
+            nc.scalar.activation(
+                out=squares[:], in_=pre[:], func=ACT.Square, bias=neg_mu[:], accum_out=dev_sq[:]
+            )
+            rstd = small("rstd")
+            nc.gpsimd.tensor_scalar(
+                out=rstd[:], in0=dev_sq[:], scalar1=1.0 / H, scalar2=LN_EPS, op0=ALU.mult, op1=ALU.add
+            )
+            nc.gpsimd.tensor_tensor(out=rstd[:], in0=rstd[:], in1=neg_half[:], op=ALU.pow)
+
+            centred = big("centred")
+            nc.vector.scalar_tensor_tensor(
+                out=centred[:], in0=pre[:], scalar=neg_mu[:], in1=gain[t][:], op0=ALU.add, op1=ALU.mult
+            )
+            shift_c = big("shift_c")
+            nc.vector.scalar_tensor_tensor(
+                out=shift_c[:], in0=centred[:], scalar=rstd[:], in1=rest[t][:], op0=ALU.mult, op1=ALU.add
+            )
+            nc.sync.dma_start(out=by_row_tile(out_1)[:, t, :], in_=shift_c[:])
+
+            squashed = big("squashed")
+            nc.scalar.activation(out=squashed[:], in_=shift_c[:], func=ACT.Tanh)
+            h_out = big("h_out")
+            nc.vector.tensor_tensor(out=h_out[:], in0=squashed[:], in1=o_sb[:, t, :], op=ALU.mult)
+            nc.sync.dma_start(out=by_row_tile(out_0)[:, t, :], in_=h_out[:])

@@ -49,24 +49,24 @@ def tile_bag_lstm_pb_s_kernel(
     with ExitStack() as ctx:
         keep = ctx.enter_context(tc.tile_pool(name="keep", bufs=1))
         psum = ctx.enter_context(tc.psum_pool(name="psum", bufs=1))
+        ctx.enter_context(tc.manual_schedule())
 
-        w_scales = keep.tile([P, 3, H], U8, align_bytes=64)
-        nc.vector.memset(w_scales[:].rearrange("p g n -> p (g n)").bitcast(I32), 0)
-        warm = keep.tile([P, 1], F32)
-        nc.vector.memset(warm[:], 0.0)
-        nc.scalar.activation(out=warm[:], in_=warm[:], func=ACT.Tanh)
-        ident = keep.tile([P, P], F32)
-        make_identity(nc, ident[:])
-        half = keep.tile([P, ROW_TILES], F32)
-        nc.gpsimd.memset(half[:], 0.5)
-        neg_half = keep.tile([P, 1], F32)
-        nc.gpsimd.memset(neg_half[:], -0.5)
+        def big(name, t):
+            return keep.tile([P, H], F32, name="%s%d" % (name, t))
+
+        def small(name, t):
+            return keep.tile([P, 1], F32, name="%s%d" % (name, t))
 
         main_sb = keep.tile([P, ROW_TILES, H], BF16)
         nc.sync.dma_start(out=main_sb[:], in_=by_row_tile(main))
         branch_sb = keep.tile([P, ROW_TILES, H], BF16)
         nc.sync.dma_start(out=branch_sb[:], in_=by_row_tile(branch))
+        b_mb_all = keep.tile([P, H], BF16)
+        nc.scalar.dma_start(out=b_mb_all[:], in_=b_mb.partition_broadcast(P))
+
         w_words = keep.tile([P, 3, 2 * H], U8, align_bytes=64)
+        w_scales = keep.tile([P, 3, H], U8, align_bytes=64)
+        nc.vector.memset(w_scales[:].rearrange("p w n -> p (w n)").bitcast(I32), 0)
         nc.sync.dma_start(
             out=w_words[:, 0:2, :].bitcast(I32),
             in_=W_mb_words.rearrange("g p n -> p g n").bitcast(I32),
@@ -79,43 +79,49 @@ def tile_bag_lstm_pb_s_kernel(
         nc.sync.dma_start(out=w_words[:, 2, :].bitcast(I32), in_=W_b_words[0].bitcast(I32))
         for r in range(4):
             nc.sync.dma_start(
-                out=w_scales[r:P:32, 2, :].bitcast(I32),
-                in_=W_b_scales[0, r:16:4, :].bitcast(I32),
+                out=w_scales[r:P:32, 2, :].bitcast(I32), in_=W_b_scales[0, r:16:4, :].bitcast(I32)
             )
-        o_sb = keep.tile([P, ROW_TILES, H], BF16)
-        nc.sync.dma_start(out=o_sb[:], in_=by_row_tile(o))
+        b_b_all = keep.tile([P, H], BF16)
+        nc.sync.dma_start(out=b_b_all[:], in_=b_b.partition_broadcast(P))
+
+        warm = keep.tile([P, 1], F32)
+        nc.vector.memset(warm[:], 0.0)
+        nc.scalar.activation(out=warm[:], in_=warm[:], func=ACT.Tanh)
+        ident = keep.tile([P, P], F32)
+        make_identity(nc, ident[:])
+        half = keep.tile([P, ROW_TILES], F32)
+        nc.gpsimd.memset(half[:], 0.5)
+        neg_half = keep.tile([P, 1], F32)
+        nc.gpsimd.memset(neg_half[:], -0.5)
 
         bag_bf = keep.tile([P, ROW_TILES], BF16)
         nc.gpsimd.dma_start(out=bag_bf[:], in_=is_bag.rearrange("(p t) one -> p (t one)", t=ROW_TILES))
         ln_b_all = keep.tile([P, H], BF16)
         nc.gpsimd.dma_start(out=ln_b_all[:], in_=ln_b.partition_broadcast(P))
-        b_mb_all = keep.tile([P, H], BF16)
-        nc.gpsimd.dma_start(out=b_mb_all[:], in_=b_mb.partition_broadcast(P))
-        b_b_all = keep.tile([P, H], BF16)
-        nc.gpsimd.dma_start(out=b_b_all[:], in_=b_b.partition_broadcast(P))
         ln_g_all = keep.tile([P, H], BF16)
         nc.gpsimd.dma_start(out=ln_g_all[:], in_=ln_g.partition_broadcast(P))
+        o_sb = keep.tile([P, ROW_TILES, H], BF16)
+        nc.gpsimd.dma_start(out=o_sb[:], in_=by_row_tile(o))
 
         x_codes = keep.tile([P, 2, B], U32, align_bytes=64)
         x_scales = keep.tile([P, 2, B], U8, align_bytes=64)
-        grouped = []
-        for g, x_sb in enumerate((main_sb, branch_sb)):
+
+        def flip(g, x_sb, copy_out):
             flipped = psum.tile([P, 2, B], F32, name="flipped%d" % g)
             for t in range(ROW_TILES):
                 words = x_sb[:, t, :].bitcast(F32)
                 for u in range(2):
                     nc.tensor.transpose(flipped[:, u, t * P : (t + 1) * P], words[:, u:WORDS:2], ident[:])
-            side_by_side = keep.tile([P, 4 * B], BF16, align_bytes=64, name="grouped%d" % g)
-            dst = side_by_side[:].bitcast(F32).rearrange("p (c u) -> p c u", u=2)
-            src = flipped[:].rearrange("p u c -> p c u")
-            if g == 0:
-                nc.vector.tensor_copy(out=dst, in_=src)
-            else:
-                nc.scalar.copy(out=dst, in_=src)
-            grouped.append(side_by_side)
-        for g in range(2):
+            grouped = keep.tile([P, 4 * B], BF16, align_bytes=64, name="grouped%d" % g)
+            copy_out(
+                out=grouped[:].bitcast(F32).rearrange("p (c u) -> p c u", u=2),
+                in_=flipped[:].rearrange("p u c -> p c u"),
+            )
+            return grouped
+
+        def quantise(g, grouped):
             nc.vector.quantize_mx(
-                out=x_codes[:, g, :].bitcast(FP8X4), scales=x_scales[:, g, :], in_=grouped[g][:]
+                out=x_codes[:, g, :].bitcast(FP8X4), scales=x_scales[:, g, :], in_=grouped[:]
             )
 
         def mx_pass(acc, t, g, w, start, stop):
@@ -130,110 +136,124 @@ def tile_bag_lstm_pb_s_kernel(
                 stop=stop,
             )
 
-        gate_acc = []
-        lin_acc = []
-        for t in range(ROW_TILES):
-            gate = psum.tile([P, H], F32, name="gate_acc%d" % t)
-            mx_pass(gate, t, 0, 0, True, False)
-            mx_pass(gate, t, 1, 1, False, True)
-            lin = psum.tile([P, H], F32, name="lin_acc%d" % t)
-            mx_pass(lin, t, 1, 2, True, True)
-            gate_acc.append(gate)
-            lin_acc.append(lin)
+        gate_acc = [psum.tile([P, H], F32, name="gate_acc%d" % t) for t in range(ROW_TILES)]
+        lin_acc = [psum.tile([P, H], F32, name="lin_acc%d" % t) for t in range(ROW_TILES)]
 
-        bag = keep.tile([P, ROW_TILES], F32)
-        nc.vector.tensor_copy(out=bag[:], in_=bag_bf[:])
-        one_minus_bag = keep.tile([P, ROW_TILES], F32)
-        nc.vector.tensor_scalar(
-            out=one_minus_bag[:], in0=bag[:], scalar1=-1.0, scalar2=1.0, op0=ALU.mult, op1=ALU.add
-        )
+        main_grouped = flip(0, main_sb, nc.vector.tensor_copy)
+        branch_grouped = flip(1, branch_sb, nc.scalar.copy)
+        quantise(0, main_grouped)
+        for t in range(ROW_TILES):
+            mx_pass(gate_acc[t], t, 0, 0, True, False)
+        quantise(1, branch_grouped)
+        for t in range(ROW_TILES):
+            mx_pass(gate_acc[t], t, 1, 1, False, True)
+            mx_pass(lin_acc[t], t, 1, 2, True, True)
+
         squares = keep.tile([P, H], F32)
         em_sq = keep.tile([P, ROW_TILES], F32)
-        gain = []
-        rest = []
         for t in range(ROW_TILES):
-            col = slice(t, t + 1)
             nc.scalar.activation(
-                out=squares[:], in_=main_sb[:, t, :], func=ACT.Square, accum_out=em_sq[:, col]
+                out=squares[:], in_=main_sb[:, t, :], func=ACT.Square, accum_out=em_sq[:, t : t + 1]
             )
-            kept = keep.tile([P, H], F32, name="kept%d" % t)
-            nc.scalar.activation(out=kept[:], in_=main_sb[:, t, :], func=ACT.Copy, scale=one_minus_bag[:, col])
-            rest_t = keep.tile([P, H], F32, name="rest%d" % t)
-            nc.vector.scalar_tensor_tensor(
-                out=rest_t[:], in0=ln_b_all[:], scalar=bag[:, col], in1=kept[:], op0=ALU.mult, op1=ALU.add
-            )
-            gain_t = keep.tile([P, H], F32, name="gain%d" % t)
-            nc.scalar.activation(out=gain_t[:], in_=ln_g_all[:], func=ACT.Copy, scale=bag[:, col])
-            gain.append(gain_t)
-            rest.append(rest_t)
         em = keep.tile([P, ROW_TILES], F32)
         nc.gpsimd.tensor_tensor(out=em[:], in0=em_sq[:], in1=half[:], op=ALU.pow)
 
-        for t in range(ROW_TILES):
-            col = slice(t, t + 1)
+        h_m = [big("h_m", t) for t in range(ROW_TILES)]
+        hm = [small("hm", t) for t in range(ROW_TILES)]
 
-            def big(name):
-                return keep.tile([P, H], F32, name="%s%d" % (name, t))
-
-            def small(name):
-                return keep.tile([P, 1], F32, name="%s%d" % (name, t))
-
-            gate_b = big("gate_b")
+        def product(t):
+            gate_b = big("gate_b", t)
             nc.vector.tensor_tensor(out=gate_b[:], in0=gate_acc[t][:], in1=b_mb_all[:], op=ALU.add)
-            lin_b = big("lin_b")
+            lin_b = big("lin_b", t)
             nc.vector.tensor_tensor(out=lin_b[:], in0=lin_acc[t][:], in1=b_b_all[:], op=ALU.add)
-            h_m = big("h_m")
             nc.vector.scalar_tensor_tensor(
-                out=h_m[:], in0=gate_b[:], scalar=0.0, in1=lin_b[:], op0=ALU.max, op1=ALU.mult
+                out=h_m[t][:], in0=gate_b[:], scalar=0.0, in1=lin_b[:], op0=ALU.max, op1=ALU.mult
             )
+            hm_sq = small("hm_sq", t)
+            nc.scalar.activation(out=squares[:], in_=h_m[t][:], func=ACT.Square, accum_out=hm_sq[:])
+            nc.gpsimd.tensor_tensor(out=hm[t][:], in0=hm_sq[:], in1=half[:, 0:1], op=ALU.pow)
 
-            hm_sq = small("hm_sq")
-            nc.scalar.activation(out=squares[:], in_=h_m[:], func=ACT.Square, accum_out=hm_sq[:])
-            hm = small("hm")
-            nc.gpsimd.tensor_tensor(out=hm[:], in0=hm_sq[:], in1=half[:, 0:1], op=ALU.pow)
-            alpha = small("alpha")
-            nc.vector.tensor_scalar_add(out=alpha[:], in0=hm[:], scalar1=BAG_EPS)
+        pre = [big("pre", t) for t in range(ROW_TILES)]
+        neg_mu = [small("neg_mu", t) for t in range(ROW_TILES)]
+        dev_sq = [small("dev_sq", t) for t in range(ROW_TILES)]
+
+        def clip(t):
+            alpha = small("alpha", t)
+            nc.vector.tensor_scalar_add(out=alpha[:], in0=hm[t][:], scalar1=BAG_EPS)
             nc.vector.reciprocal(out=alpha[:], in_=alpha[:])
             nc.vector.tensor_scalar(
-                out=alpha[:], in0=alpha[:], scalar1=em[:, col], scalar2=1.0, op0=ALU.mult, op1=ALU.min
+                out=alpha[:], in0=alpha[:], scalar1=em[:, t : t + 1], scalar2=1.0, op0=ALU.mult, op1=ALU.min
             )
-
-            pre = big("pre")
-            pre_sum = small("pre_sum")
+            pre_sum = small("pre_sum", t)
             nc.vector.scalar_tensor_tensor(
-                out=pre[:],
-                in0=h_m[:],
+                out=pre[t][:],
+                in0=h_m[t][:],
                 scalar=alpha[:],
                 in1=main_sb[:, t, :],
                 op0=ALU.mult,
                 op1=ALU.add,
                 accum_out=pre_sum[:],
             )
-            neg_mu = small("neg_mu")
-            nc.vector.tensor_scalar_mul(out=neg_mu[:], in0=pre_sum[:], scalar1=-1.0 / H)
-
-            dev_sq = small("dev_sq")
+            nc.vector.tensor_scalar_mul(out=neg_mu[t][:], in0=pre_sum[:], scalar1=-1.0 / H)
             nc.scalar.activation(
-                out=squares[:], in_=pre[:], func=ACT.Square, bias=neg_mu[:], accum_out=dev_sq[:]
+                out=squares[:], in_=pre[t][:], func=ACT.Square, bias=neg_mu[t][:], accum_out=dev_sq[t][:]
             )
-            rstd = small("rstd")
-            nc.gpsimd.tensor_scalar(
-                out=rstd[:], in0=dev_sq[:], scalar1=1.0 / H, scalar2=LN_EPS, op0=ALU.mult, op1=ALU.add
-            )
-            nc.gpsimd.tensor_tensor(out=rstd[:], in0=rstd[:], in1=neg_half[:], op=ALU.pow)
 
-            centred = big("centred")
-            nc.vector.scalar_tensor_tensor(
-                out=centred[:], in0=pre[:], scalar=neg_mu[:], in1=gain[t][:], op0=ALU.add, op1=ALU.mult
-            )
-            shift_c = big("shift_c")
-            nc.vector.scalar_tensor_tensor(
-                out=shift_c[:], in0=centred[:], scalar=rstd[:], in1=rest[t][:], op0=ALU.mult, op1=ALU.add
-            )
-            nc.sync.dma_start(out=by_row_tile(out_1)[:, t, :], in_=shift_c[:])
+        bag = keep.tile([P, ROW_TILES], F32)
+        one_minus_bag = keep.tile([P, ROW_TILES], F32)
+        kept = [big("kept", t) for t in range(ROW_TILES)]
+        gain = [big("gain", t) for t in range(ROW_TILES)]
+        rest = [big("rest", t) for t in range(ROW_TILES)]
+        centred = [big("centred", t) for t in range(ROW_TILES)]
+        rstd = [small("rstd", t) for t in range(ROW_TILES)]
+        shift_c = [big("shift_c", t) for t in range(ROW_TILES)]
+        squashed = [big("squashed", t) for t in range(ROW_TILES)]
 
-            squashed = big("squashed")
-            nc.scalar.activation(out=squashed[:], in_=shift_c[:], func=ACT.Tanh)
-            h_out = big("h_out")
-            nc.vector.tensor_tensor(out=h_out[:], in0=squashed[:], in1=o_sb[:, t, :], op=ALU.mult)
+        def centre(t):
+            nc.vector.scalar_tensor_tensor(
+                out=centred[t][:], in0=pre[t][:], scalar=neg_mu[t][:], in1=gain[t][:], op0=ALU.add, op1=ALU.mult
+            )
+
+        def spread(t):
+            var_eps = small("var_eps", t)
+            nc.vector.tensor_scalar(
+                out=var_eps[:], in0=dev_sq[t][:], scalar1=1.0 / H, scalar2=LN_EPS, op0=ALU.mult, op1=ALU.add
+            )
+            nc.gpsimd.tensor_tensor(out=rstd[t][:], in0=var_eps[:], in1=neg_half[:], op=ALU.pow)
+
+        def blend(t):
+            nc.vector.scalar_tensor_tensor(
+                out=shift_c[t][:], in0=centred[t][:], scalar=rstd[t][:], in1=rest[t][:], op0=ALU.mult, op1=ALU.add
+            )
+            nc.sync.dma_start(out=by_row_tile(out_1)[:, t, :], in_=shift_c[t][:])
+            nc.scalar.activation(out=squashed[t][:], in_=shift_c[t][:], func=ACT.Tanh)
+
+        def gate_out(t):
+            h_out = big("h_out", t)
+            nc.vector.tensor_tensor(out=h_out[:], in0=squashed[t][:], in1=o_sb[:, t, :], op=ALU.mult)
             nc.sync.dma_start(out=by_row_tile(out_0)[:, t, :], in_=h_out[:])
+
+        product(0)
+        nc.vector.tensor_copy(out=bag[:], in_=bag_bf[:])
+        nc.vector.tensor_scalar(
+            out=one_minus_bag[:], in0=bag[:], scalar1=-1.0, scalar2=1.0, op0=ALU.mult, op1=ALU.add
+        )
+        for t in range(ROW_TILES):
+            nc.scalar.activation(
+                out=kept[t][:], in_=main_sb[:, t, :], func=ACT.Copy, scale=one_minus_bag[:, t : t + 1]
+            )
+        for t in range(ROW_TILES):
+            nc.scalar.activation(out=gain[t][:], in_=ln_g_all[:], func=ACT.Copy, scale=bag[:, t : t + 1])
+        product(1)
+        for t in range(ROW_TILES):
+            nc.vector.scalar_tensor_tensor(
+                out=rest[t][:], in0=ln_b_all[:], scalar=bag[:, t : t + 1], in1=kept[t][:], op0=ALU.mult, op1=ALU.add
+            )
+        for t in range(ROW_TILES):
+            clip(t)
+            centre(t)
+            spread(t)
+        for t in range(ROW_TILES):
+            blend(t)
+        for t in range(ROW_TILES):
+            gate_out(t)

@@ -42,27 +42,31 @@ def tile_bag_lstm_pb_s_kernel(
     out_1,
 ):
     nc = tc.nc
+    tiles = range(ROW_TILES)
 
     def by_row_tile(ap):
         return ap.rearrange("(p t) c -> p t c", t=ROW_TILES)
+
+    def col(per_row, t):
+        return per_row[:, t : t + 1]
 
     with ExitStack() as ctx:
         keep = ctx.enter_context(tc.tile_pool(name="keep", bufs=1))
         psum = ctx.enter_context(tc.psum_pool(name="psum", bufs=1))
         ctx.enter_context(tc.manual_schedule())
 
-        def big(name, t):
-            return keep.tile([P, H], F32, name="%s%d" % (name, t))
+        def big(name):
+            return [keep.tile([P, H], F32, name="%s%d" % (name, t)) for t in tiles]
 
-        def small(name, t):
-            return keep.tile([P, 1], F32, name="%s%d" % (name, t))
+        def per_row(name):
+            return keep.tile([P, ROW_TILES], F32, name=name)
 
         main_sb = keep.tile([P, ROW_TILES, H], BF16)
         nc.sync.dma_start(out=main_sb[:], in_=by_row_tile(main))
         branch_sb = keep.tile([P, ROW_TILES, H], BF16)
         nc.sync.dma_start(out=branch_sb[:], in_=by_row_tile(branch))
-        b_mb_all = keep.tile([P, H], BF16)
-        nc.scalar.dma_start(out=b_mb_all[:], in_=b_mb.partition_broadcast(P))
+        bag_bf = keep.tile([P, ROW_TILES], BF16)
+        nc.sync.dma_start(out=bag_bf[:], in_=is_bag.rearrange("(p t) one -> p (t one)", t=ROW_TILES))
 
         w_words = keep.tile([P, 3, 2 * H], U8, align_bytes=64)
         w_scales = keep.tile([P, 3, H], U8, align_bytes=64)
@@ -81,21 +85,13 @@ def tile_bag_lstm_pb_s_kernel(
             nc.sync.dma_start(
                 out=w_scales[r:P:32, 2, :].bitcast(I32), in_=W_b_scales[0, r:16:4, :].bitcast(I32)
             )
-        b_b_all = keep.tile([P, H], BF16)
-        nc.sync.dma_start(out=b_b_all[:], in_=b_b.partition_broadcast(P))
 
-        warm = keep.tile([P, 1], F32)
-        nc.vector.memset(warm[:], 0.0)
-        nc.scalar.activation(out=warm[:], in_=warm[:], func=ACT.Tanh)
+        bias_rows = keep.tile([P, 2, H], BF16)
+        nc.vector.memset(bias_rows[:].rearrange("p v c -> p (v c)").bitcast(I32), 0)
+        nc.gpsimd.dma_start(out=bias_rows[0:1, 0, :], in_=b_mb.unsqueeze(0))
+        nc.gpsimd.dma_start(out=bias_rows[0:1, 1, :], in_=b_b.unsqueeze(0))
         ident = keep.tile([P, P], F32)
         make_identity(nc, ident[:])
-        half = keep.tile([P, ROW_TILES], F32)
-        nc.gpsimd.memset(half[:], 0.5)
-        neg_half = keep.tile([P, 1], F32)
-        nc.gpsimd.memset(neg_half[:], -0.5)
-
-        bag_bf = keep.tile([P, ROW_TILES], BF16)
-        nc.gpsimd.dma_start(out=bag_bf[:], in_=is_bag.rearrange("(p t) one -> p (t one)", t=ROW_TILES))
         ln_b_all = keep.tile([P, H], BF16)
         nc.gpsimd.dma_start(out=ln_b_all[:], in_=ln_b.partition_broadcast(P))
         ln_g_all = keep.tile([P, H], BF16)
@@ -103,12 +99,22 @@ def tile_bag_lstm_pb_s_kernel(
         o_sb = keep.tile([P, ROW_TILES, H], BF16)
         nc.gpsimd.dma_start(out=o_sb[:], in_=by_row_tile(o))
 
+        ones = keep.tile([P, P], BF16)
+        nc.vector.memset(ones[:], 1.0)
+        warm = keep.tile([P, 1], F32)
+        nc.vector.memset(warm[:], 0.0)
+        nc.scalar.activation(out=warm[:], in_=warm[:], func=ACT.Tanh)
+        half = per_row("half")
+        nc.gpsimd.memset(half[:], 0.5)
+        neg_half = per_row("neg_half")
+        nc.gpsimd.memset(neg_half[:], -0.5)
+
         x_codes = keep.tile([P, 2, B], U32, align_bytes=64)
         x_scales = keep.tile([P, 2, B], U8, align_bytes=64)
 
         def flip(g, x_sb, copy_out):
             flipped = psum.tile([P, 2, B], F32, name="flipped%d" % g)
-            for t in range(ROW_TILES):
+            for t in tiles:
                 words = x_sb[:, t, :].bitcast(F32)
                 for u in range(2):
                     nc.tensor.transpose(flipped[:, u, t * P : (t + 1) * P], words[:, u:WORDS:2], ident[:])
@@ -136,124 +142,110 @@ def tile_bag_lstm_pb_s_kernel(
                 stop=stop,
             )
 
-        gate_acc = [psum.tile([P, H], F32, name="gate_acc%d" % t) for t in range(ROW_TILES)]
-        lin_acc = [psum.tile([P, H], F32, name="lin_acc%d" % t) for t in range(ROW_TILES)]
+        gate_acc = [psum.tile([P, H], F32, name="gate_acc%d" % t) for t in tiles]
+        lin_acc = [psum.tile([P, H], F32, name="lin_acc%d" % t) for t in tiles]
 
         main_grouped = flip(0, main_sb, nc.vector.tensor_copy)
         branch_grouped = flip(1, branch_sb, nc.scalar.copy)
+
+        bias_all = [keep.tile([P, H], F32, name="bias_all%d" % v) for v in range(2)]
+        for v in range(2):
+            spread_out = psum.tile([P, H], F32, name="spread_out%d" % v)
+            nc.tensor.matmul(out=spread_out[:], lhsT=ones[:], rhs=bias_rows[:, v, :], start=True, stop=True)
+            nc.scalar.copy(out=bias_all[v][:], in_=spread_out[:])
+
         quantise(0, main_grouped)
-        for t in range(ROW_TILES):
+        for t in tiles:
             mx_pass(gate_acc[t], t, 0, 0, True, False)
         quantise(1, branch_grouped)
-        for t in range(ROW_TILES):
+        for t in tiles:
             mx_pass(gate_acc[t], t, 1, 1, False, True)
             mx_pass(lin_acc[t], t, 1, 2, True, True)
 
         squares = keep.tile([P, H], F32)
-        em_sq = keep.tile([P, ROW_TILES], F32)
-        for t in range(ROW_TILES):
-            nc.scalar.activation(
-                out=squares[:], in_=main_sb[:, t, :], func=ACT.Square, accum_out=em_sq[:, t : t + 1]
-            )
-        em = keep.tile([P, ROW_TILES], F32)
+        em_sq = per_row("em_sq")
+        for t in tiles:
+            nc.scalar.activation(out=squares[:], in_=main_sb[:, t, :], func=ACT.Square, accum_out=col(em_sq, t))
+        em = per_row("em")
         nc.gpsimd.tensor_tensor(out=em[:], in0=em_sq[:], in1=half[:], op=ALU.pow)
 
-        h_m = [big("h_m", t) for t in range(ROW_TILES)]
-        hm = [small("hm", t) for t in range(ROW_TILES)]
-
-        def product(t):
-            gate_b = big("gate_b", t)
-            nc.vector.tensor_tensor(out=gate_b[:], in0=gate_acc[t][:], in1=b_mb_all[:], op=ALU.add)
-            lin_b = big("lin_b", t)
-            nc.vector.tensor_tensor(out=lin_b[:], in0=lin_acc[t][:], in1=b_b_all[:], op=ALU.add)
-            nc.vector.scalar_tensor_tensor(
-                out=h_m[t][:], in0=gate_b[:], scalar=0.0, in1=lin_b[:], op0=ALU.max, op1=ALU.mult
-            )
-            hm_sq = small("hm_sq", t)
-            nc.scalar.activation(out=squares[:], in_=h_m[t][:], func=ACT.Square, accum_out=hm_sq[:])
-            nc.gpsimd.tensor_tensor(out=hm[t][:], in0=hm_sq[:], in1=half[:, 0:1], op=ALU.pow)
-
-        pre = [big("pre", t) for t in range(ROW_TILES)]
-        neg_mu = [small("neg_mu", t) for t in range(ROW_TILES)]
-        dev_sq = [small("dev_sq", t) for t in range(ROW_TILES)]
-
-        def clip(t):
-            alpha = small("alpha", t)
-            nc.vector.tensor_scalar_add(out=alpha[:], in0=hm[t][:], scalar1=BAG_EPS)
-            nc.vector.reciprocal(out=alpha[:], in_=alpha[:])
-            nc.vector.tensor_scalar(
-                out=alpha[:], in0=alpha[:], scalar1=em[:, t : t + 1], scalar2=1.0, op0=ALU.mult, op1=ALU.min
-            )
-            pre_sum = small("pre_sum", t)
-            nc.vector.scalar_tensor_tensor(
-                out=pre[t][:],
-                in0=h_m[t][:],
-                scalar=alpha[:],
-                in1=main_sb[:, t, :],
-                op0=ALU.mult,
-                op1=ALU.add,
-                accum_out=pre_sum[:],
-            )
-            nc.vector.tensor_scalar_mul(out=neg_mu[t][:], in0=pre_sum[:], scalar1=-1.0 / H)
-            nc.scalar.activation(
-                out=squares[:], in_=pre[t][:], func=ACT.Square, bias=neg_mu[t][:], accum_out=dev_sq[t][:]
-            )
-
-        bag = keep.tile([P, ROW_TILES], F32)
-        one_minus_bag = keep.tile([P, ROW_TILES], F32)
-        kept = [big("kept", t) for t in range(ROW_TILES)]
-        gain = [big("gain", t) for t in range(ROW_TILES)]
-        rest = [big("rest", t) for t in range(ROW_TILES)]
-        centred = [big("centred", t) for t in range(ROW_TILES)]
-        rstd = [small("rstd", t) for t in range(ROW_TILES)]
-        shift_c = [big("shift_c", t) for t in range(ROW_TILES)]
-        squashed = [big("squashed", t) for t in range(ROW_TILES)]
-
-        def centre(t):
-            nc.vector.scalar_tensor_tensor(
-                out=centred[t][:], in0=pre[t][:], scalar=neg_mu[t][:], in1=gain[t][:], op0=ALU.add, op1=ALU.mult
-            )
-
-        def spread(t):
-            var_eps = small("var_eps", t)
-            nc.vector.tensor_scalar(
-                out=var_eps[:], in0=dev_sq[t][:], scalar1=1.0 / H, scalar2=LN_EPS, op0=ALU.mult, op1=ALU.add
-            )
-            nc.gpsimd.tensor_tensor(out=rstd[t][:], in0=var_eps[:], in1=neg_half[:], op=ALU.pow)
-
-        def blend(t):
-            nc.vector.scalar_tensor_tensor(
-                out=shift_c[t][:], in0=centred[t][:], scalar=rstd[t][:], in1=rest[t][:], op0=ALU.mult, op1=ALU.add
-            )
-            nc.sync.dma_start(out=by_row_tile(out_1)[:, t, :], in_=shift_c[t][:])
-            nc.scalar.activation(out=squashed[t][:], in_=shift_c[t][:], func=ACT.Tanh)
-
-        def gate_out(t):
-            h_out = big("h_out", t)
-            nc.vector.tensor_tensor(out=h_out[:], in0=squashed[t][:], in1=o_sb[:, t, :], op=ALU.mult)
-            nc.sync.dma_start(out=by_row_tile(out_0)[:, t, :], in_=h_out[:])
-
-        product(0)
+        bag = per_row("bag")
         nc.vector.tensor_copy(out=bag[:], in_=bag_bf[:])
+        one_minus_bag = per_row("one_minus_bag")
         nc.vector.tensor_scalar(
             out=one_minus_bag[:], in0=bag[:], scalar1=-1.0, scalar2=1.0, op0=ALU.mult, op1=ALU.add
         )
-        for t in range(ROW_TILES):
-            nc.scalar.activation(
-                out=kept[t][:], in_=main_sb[:, t, :], func=ACT.Copy, scale=one_minus_bag[:, t : t + 1]
-            )
-        for t in range(ROW_TILES):
-            nc.scalar.activation(out=gain[t][:], in_=ln_g_all[:], func=ACT.Copy, scale=bag[:, t : t + 1])
-        product(1)
-        for t in range(ROW_TILES):
+        kept = big("kept")
+        for t in tiles:
+            nc.scalar.activation(out=kept[t][:], in_=main_sb[:, t, :], func=ACT.Copy, scale=col(one_minus_bag, t))
+
+        gate_b = big("gate_b")
+        lin_b = big("lin_b")
+        h_m = big("h_m")
+        hm_sq = per_row("hm_sq")
+        gain = big("gain")
+        for t in tiles:
+            nc.vector.tensor_tensor(out=gate_b[t][:], in0=gate_acc[t][:], in1=bias_all[0][:], op=ALU.add)
+            nc.vector.tensor_tensor(out=lin_b[t][:], in0=lin_acc[t][:], in1=bias_all[1][:], op=ALU.add)
             nc.vector.scalar_tensor_tensor(
-                out=rest[t][:], in0=ln_b_all[:], scalar=bag[:, t : t + 1], in1=kept[t][:], op0=ALU.mult, op1=ALU.add
+                out=h_m[t][:], in0=gate_b[t][:], scalar=0.0, in1=lin_b[t][:], op0=ALU.max, op1=ALU.mult
             )
-        for t in range(ROW_TILES):
-            clip(t)
-            centre(t)
-            spread(t)
-        for t in range(ROW_TILES):
-            blend(t)
-        for t in range(ROW_TILES):
-            gate_out(t)
+            nc.scalar.activation(out=squares[:], in_=h_m[t][:], func=ACT.Square, accum_out=col(hm_sq, t))
+            nc.scalar.activation(out=gain[t][:], in_=ln_g_all[:], func=ACT.Copy, scale=col(bag, t))
+        hm = per_row("hm")
+        nc.gpsimd.tensor_tensor(out=hm[:], in0=hm_sq[:], in1=half[:], op=ALU.pow)
+
+        rest = big("rest")
+        for t in tiles:
+            nc.vector.scalar_tensor_tensor(
+                out=rest[t][:], in0=ln_b_all[:], scalar=col(bag, t), in1=kept[t][:], op0=ALU.mult, op1=ALU.add
+            )
+
+        alpha = per_row("alpha")
+        nc.vector.scalar_tensor_tensor(
+            out=alpha[:], in0=hm[:], scalar=BAG_EPS, in1=em[:], op0=ALU.add, op1=ALU.max
+        )
+        nc.vector.reciprocal(out=alpha[:], in_=alpha[:])
+        nc.vector.tensor_tensor(out=alpha[:], in0=alpha[:], in1=em[:], op=ALU.mult)
+
+        pre = big("pre")
+        pre_sum = per_row("pre_sum")
+        neg_mu = per_row("neg_mu")
+        dev_sq = per_row("dev_sq")
+        for t in tiles:
+            nc.vector.scalar_tensor_tensor(
+                out=pre[t][:],
+                in0=h_m[t][:],
+                scalar=col(alpha, t),
+                in1=main_sb[:, t, :],
+                op0=ALU.mult,
+                op1=ALU.add,
+                accum_out=col(pre_sum, t),
+            )
+            nc.vector.tensor_scalar_mul(out=col(neg_mu, t), in0=col(pre_sum, t), scalar1=-1.0 / H)
+            nc.scalar.activation(
+                out=squares[:], in_=pre[t][:], func=ACT.Square, bias=col(neg_mu, t), accum_out=col(dev_sq, t)
+            )
+        centred = big("centred")
+        for t in tiles:
+            nc.vector.scalar_tensor_tensor(
+                out=centred[t][:], in0=pre[t][:], scalar=col(neg_mu, t), in1=gain[t][:], op0=ALU.add, op1=ALU.mult
+            )
+        rstd = per_row("rstd")
+        nc.vector.tensor_scalar(
+            out=rstd[:], in0=dev_sq[:], scalar1=1.0 / H, scalar2=LN_EPS, op0=ALU.mult, op1=ALU.add
+        )
+        nc.gpsimd.tensor_tensor(out=rstd[:], in0=rstd[:], in1=neg_half[:], op=ALU.pow)
+
+        shift_c = big("shift_c")
+        squashed = big("squashed")
+        h_out = big("h_out")
+        for t in tiles:
+            nc.vector.scalar_tensor_tensor(
+                out=shift_c[t][:], in0=centred[t][:], scalar=col(rstd, t), in1=rest[t][:], op0=ALU.mult, op1=ALU.add
+            )
+            nc.sync.dma_start(out=by_row_tile(out_1)[:, t, :], in_=shift_c[t][:])
+            nc.scalar.activation(out=squashed[t][:], in_=shift_c[t][:], func=ACT.Tanh)
+        for t in tiles:
+            nc.vector.tensor_tensor(out=h_out[t][:], in0=squashed[t][:], in1=o_sb[:, t, :], op=ALU.mult)
+            nc.sync.dma_start(out=by_row_tile(out_0)[:, t, :], in_=h_out[t][:])

@@ -61,13 +61,15 @@ def tile_bag_lstm_pb_s_kernel(
         def per_row(name):
             return keep.tile([P, ROW_TILES], F32, name=name)
 
+        bias_rows = keep.tile([P, 2, H], BF16)
+        nc.vector.memset(bias_rows[:].rearrange("p v c -> p (v c)").bitcast(I32), 0)
+        nc.scalar.dma_start(out=bias_rows[0:1, 0, :], in_=b_mb.unsqueeze(0))
+        nc.scalar.dma_start(out=bias_rows[0:1, 1, :], in_=b_b.unsqueeze(0))
+
         main_sb = keep.tile([P, ROW_TILES, H], BF16)
         nc.sync.dma_start(out=main_sb[:], in_=by_row_tile(main))
         branch_sb = keep.tile([P, ROW_TILES, H], BF16)
         nc.sync.dma_start(out=branch_sb[:], in_=by_row_tile(branch))
-        bag_bf = keep.tile([P, ROW_TILES], BF16)
-        nc.sync.dma_start(out=bag_bf[:], in_=is_bag.rearrange("(p t) one -> p (t one)", t=ROW_TILES))
-
         w_words = keep.tile([P, 3, 2 * H], U8, align_bytes=64)
         w_scales = keep.tile([P, 3, H], U8, align_bytes=64)
         nc.vector.memset(w_scales[:].rearrange("p w n -> p (w n)").bitcast(I32), 0)
@@ -86,12 +88,10 @@ def tile_bag_lstm_pb_s_kernel(
                 out=w_scales[r:P:32, 2, :].bitcast(I32), in_=W_b_scales[0, r:16:4, :].bitcast(I32)
             )
 
-        bias_rows = keep.tile([P, 2, H], BF16)
-        nc.vector.memset(bias_rows[:].rearrange("p v c -> p (v c)").bitcast(I32), 0)
-        nc.gpsimd.dma_start(out=bias_rows[0:1, 0, :], in_=b_mb.unsqueeze(0))
-        nc.gpsimd.dma_start(out=bias_rows[0:1, 1, :], in_=b_b.unsqueeze(0))
         ident = keep.tile([P, P], F32)
         make_identity(nc, ident[:])
+        bag_bf = keep.tile([P, ROW_TILES], BF16)
+        nc.gpsimd.dma_start(out=bag_bf[:], in_=is_bag.rearrange("(p t) one -> p (t one)", t=ROW_TILES))
         ln_b_all = keep.tile([P, H], BF16)
         nc.gpsimd.dma_start(out=ln_b_all[:], in_=ln_b.partition_broadcast(P))
         ln_g_all = keep.tile([P, H], BF16)
@@ -145,22 +145,30 @@ def tile_bag_lstm_pb_s_kernel(
         gate_acc = [psum.tile([P, H], F32, name="gate_acc%d" % t) for t in tiles]
         lin_acc = [psum.tile([P, H], F32, name="lin_acc%d" % t) for t in tiles]
 
-        main_grouped = flip(0, main_sb, nc.vector.tensor_copy)
-        branch_grouped = flip(1, branch_sb, nc.scalar.copy)
-
         bias_all = [keep.tile([P, H], F32, name="bias_all%d" % v) for v in range(2)]
-        for v in range(2):
+
+        def spread_bias(v, copy_out):
             spread_out = psum.tile([P, H], F32, name="spread_out%d" % v)
             nc.tensor.matmul(out=spread_out[:], lhsT=ones[:], rhs=bias_rows[:, v, :], start=True, stop=True)
-            nc.scalar.copy(out=bias_all[v][:], in_=spread_out[:])
+            copy_out(out=bias_all[v][:], in_=spread_out[:])
 
+        main_grouped = flip(0, main_sb, nc.vector.tensor_copy)
+        branch_grouped = flip(1, branch_sb, nc.scalar.copy)
+        spread_bias(0, nc.scalar.copy)
         quantise(0, main_grouped)
+        quantise(1, branch_grouped)
+        spread_bias(1, nc.vector.tensor_copy)
         for t in tiles:
             mx_pass(gate_acc[t], t, 0, 0, True, False)
-        quantise(1, branch_grouped)
-        for t in tiles:
             mx_pass(gate_acc[t], t, 1, 1, False, True)
             mx_pass(lin_acc[t], t, 1, 2, True, True)
+
+        bag = per_row("bag")
+        nc.gpsimd.tensor_scalar(out=bag[:], in0=bag_bf[:], scalar1=1.0, scalar2=0.0, op0=ALU.mult, op1=ALU.add)
+        one_minus_bag = per_row("one_minus_bag")
+        nc.gpsimd.tensor_scalar(
+            out=one_minus_bag[:], in0=bag_bf[:], scalar1=-1.0, scalar2=1.0, op0=ALU.mult, op1=ALU.add
+        )
 
         squares = keep.tile([P, H], F32)
         em_sq = per_row("em_sq")
@@ -169,12 +177,6 @@ def tile_bag_lstm_pb_s_kernel(
         em = per_row("em")
         nc.gpsimd.tensor_tensor(out=em[:], in0=em_sq[:], in1=half[:], op=ALU.pow)
 
-        bag = per_row("bag")
-        nc.vector.tensor_copy(out=bag[:], in_=bag_bf[:])
-        one_minus_bag = per_row("one_minus_bag")
-        nc.vector.tensor_scalar(
-            out=one_minus_bag[:], in0=bag[:], scalar1=-1.0, scalar2=1.0, op0=ALU.mult, op1=ALU.add
-        )
         kept = big("kept")
         for t in tiles:
             nc.scalar.activation(out=kept[t][:], in_=main_sb[:, t, :], func=ACT.Copy, scale=col(one_minus_bag, t))
@@ -191,9 +193,10 @@ def tile_bag_lstm_pb_s_kernel(
                 out=h_m[t][:], in0=gate_b[t][:], scalar=0.0, in1=lin_b[t][:], op0=ALU.max, op1=ALU.mult
             )
             nc.scalar.activation(out=squares[:], in_=h_m[t][:], func=ACT.Square, accum_out=col(hm_sq, t))
-            nc.scalar.activation(out=gain[t][:], in_=ln_g_all[:], func=ACT.Copy, scale=col(bag, t))
         hm = per_row("hm")
         nc.gpsimd.tensor_tensor(out=hm[:], in0=hm_sq[:], in1=half[:], op=ALU.pow)
+        for t in tiles:
+            nc.scalar.activation(out=gain[t][:], in_=ln_g_all[:], func=ACT.Copy, scale=col(bag, t))
 
         rest = big("rest")
         for t in tiles:

@@ -61,15 +61,13 @@ def tile_bag_lstm_pb_s_kernel(
         def per_row(name):
             return keep.tile([P, ROW_TILES], F32, name=name)
 
-        bias_rows = keep.tile([P, 2, H], BF16)
-        nc.vector.memset(bias_rows[:].rearrange("p v c -> p (v c)").bitcast(I32), 0)
-        nc.scalar.dma_start(out=bias_rows[0:1, 0, :], in_=b_mb.unsqueeze(0))
-        nc.scalar.dma_start(out=bias_rows[0:1, 1, :], in_=b_b.unsqueeze(0))
-
         main_sb = keep.tile([P, ROW_TILES, H], BF16)
         nc.sync.dma_start(out=main_sb[:], in_=by_row_tile(main))
         branch_sb = keep.tile([P, ROW_TILES, H], BF16)
         nc.sync.dma_start(out=branch_sb[:], in_=by_row_tile(branch))
+        bag_bf = keep.tile([P, ROW_TILES], BF16)
+        nc.sync.dma_start(out=bag_bf[:], in_=is_bag.rearrange("(p t) one -> p (t one)", t=ROW_TILES))
+
         w_words = keep.tile([P, 3, 2 * H], U8, align_bytes=64)
         w_scales = keep.tile([P, 3, H], U8, align_bytes=64)
         nc.vector.memset(w_scales[:].rearrange("p w n -> p (w n)").bitcast(I32), 0)
@@ -88,10 +86,12 @@ def tile_bag_lstm_pb_s_kernel(
                 out=w_scales[r:P:32, 2, :].bitcast(I32), in_=W_b_scales[0, r:16:4, :].bitcast(I32)
             )
 
+        bias_rows = keep.tile([P, 2, H], BF16)
+        nc.vector.memset(bias_rows[:].rearrange("p v c -> p (v c)").bitcast(I32), 0)
+        nc.gpsimd.dma_start(out=bias_rows[0:1, 0, :], in_=b_mb.unsqueeze(0))
+        nc.gpsimd.dma_start(out=bias_rows[0:1, 1, :], in_=b_b.unsqueeze(0))
         ident = keep.tile([P, P], F32)
         make_identity(nc, ident[:])
-        bag_bf = keep.tile([P, ROW_TILES], BF16)
-        nc.gpsimd.dma_start(out=bag_bf[:], in_=is_bag.rearrange("(p t) one -> p (t one)", t=ROW_TILES))
         ln_b_all = keep.tile([P, H], BF16)
         nc.gpsimd.dma_start(out=ln_b_all[:], in_=ln_b.partition_broadcast(P))
         ln_g_all = keep.tile([P, H], BF16)
@@ -145,30 +145,21 @@ def tile_bag_lstm_pb_s_kernel(
         gate_acc = [psum.tile([P, H], F32, name="gate_acc%d" % t) for t in tiles]
         lin_acc = [psum.tile([P, H], F32, name="lin_acc%d" % t) for t in tiles]
 
-        bias_all = [keep.tile([P, H], F32, name="bias_all%d" % v) for v in range(2)]
-
-        def spread_bias(v, copy_out):
-            spread_out = psum.tile([P, H], F32, name="spread_out%d" % v)
-            nc.tensor.matmul(out=spread_out[:], lhsT=ones[:], rhs=bias_rows[:, v, :], start=True, stop=True)
-            copy_out(out=bias_all[v][:], in_=spread_out[:])
-
         main_grouped = flip(0, main_sb, nc.vector.tensor_copy)
         branch_grouped = flip(1, branch_sb, nc.scalar.copy)
-        spread_bias(0, nc.scalar.copy)
+
+        bias_all = [keep.tile([P, H], F32, name="bias_all%d" % v) for v in range(2)]
+        for v in range(2):
+            spread_out = psum.tile([P, H], F32, name="spread_out%d" % v)
+            nc.tensor.matmul(out=spread_out[:], lhsT=ones[:], rhs=bias_rows[:, v, :], start=True, stop=True)
+            nc.scalar.copy(out=bias_all[v][:], in_=spread_out[:])
+
         quantise(0, main_grouped)
         quantise(1, branch_grouped)
-        spread_bias(1, nc.vector.tensor_copy)
         for t in tiles:
             mx_pass(gate_acc[t], t, 0, 0, True, False)
             mx_pass(gate_acc[t], t, 1, 1, False, True)
             mx_pass(lin_acc[t], t, 1, 2, True, True)
-
-        bag = per_row("bag")
-        nc.gpsimd.tensor_scalar(out=bag[:], in0=bag_bf[:], scalar1=1.0, scalar2=0.0, op0=ALU.mult, op1=ALU.add)
-        one_minus_bag = per_row("one_minus_bag")
-        nc.gpsimd.tensor_scalar(
-            out=one_minus_bag[:], in0=bag_bf[:], scalar1=-1.0, scalar2=1.0, op0=ALU.mult, op1=ALU.add
-        )
 
         squares = keep.tile([P, H], F32)
         em_sq = per_row("em_sq")
@@ -177,6 +168,12 @@ def tile_bag_lstm_pb_s_kernel(
         em = per_row("em")
         nc.gpsimd.tensor_tensor(out=em[:], in0=em_sq[:], in1=half[:], op=ALU.pow)
 
+        bag = per_row("bag")
+        nc.vector.tensor_copy(out=bag[:], in_=bag_bf[:])
+        one_minus_bag = per_row("one_minus_bag")
+        nc.vector.tensor_scalar(
+            out=one_minus_bag[:], in0=bag[:], scalar1=-1.0, scalar2=1.0, op0=ALU.mult, op1=ALU.add
+        )
         kept = big("kept")
         for t in tiles:
             nc.scalar.activation(out=kept[t][:], in_=main_sb[:, t, :], func=ACT.Copy, scale=col(one_minus_bag, t))

@@ -17,6 +17,7 @@ P = 128
 B = 256
 H = 512
 ROW_TILES = B // P
+CH_TILES = H // P
 WORDS = H // 2
 LN_EPS = 1e-5
 BAG_EPS = 1e-6
@@ -86,10 +87,10 @@ def tile_bag_lstm_pb_s_kernel(
                 out=w_scales[r:P:32, 2, :].bitcast(I32), in_=W_b_scales[0, r:16:4, :].bitcast(I32)
             )
 
-        bias_rows = keep.tile([P, 2, H], BF16)
-        nc.vector.memset(bias_rows[:].rearrange("p v c -> p (v c)").bitcast(I32), 0)
-        nc.gpsimd.dma_start(out=bias_rows[0:1, 0, :], in_=b_mb.unsqueeze(0))
-        nc.gpsimd.dma_start(out=bias_rows[0:1, 1, :], in_=b_b.unsqueeze(0))
+        bias_rows = keep.tile([P, P], BF16)
+        nc.vector.memset(bias_rows[:].bitcast(I32), 0)
+        nc.gpsimd.dma_start(out=bias_rows[0:CH_TILES, :], in_=b_mb.rearrange("(c p) -> c p", p=P))
+        nc.gpsimd.dma_start(out=bias_rows[CH_TILES : 2 * CH_TILES, :], in_=b_b.rearrange("(c p) -> c p", p=P))
         ident = keep.tile([P, P], F32)
         make_identity(nc, ident[:])
         ln_b_all = keep.tile([P, H], BF16)
@@ -99,11 +100,11 @@ def tile_bag_lstm_pb_s_kernel(
         o_sb = keep.tile([P, ROW_TILES, H], BF16)
         nc.gpsimd.dma_start(out=o_sb[:], in_=by_row_tile(o))
 
-        ones = keep.tile([P, P], BF16)
-        nc.vector.memset(ones[:], 1.0)
         warm = keep.tile([P, 1], F32)
         nc.vector.memset(warm[:], 0.0)
         nc.scalar.activation(out=warm[:], in_=warm[:], func=ACT.Tanh)
+        pick = keep.tile([P, 2 * CH_TILES], BF16)
+        nc.vector.tensor_copy(out=pick[:], in_=ident[:, 0 : 2 * CH_TILES])
         half = per_row("half")
         nc.gpsimd.memset(half[:], 0.5)
         neg_half = per_row("neg_half")
@@ -113,7 +114,7 @@ def tile_bag_lstm_pb_s_kernel(
         x_scales = keep.tile([P, 2, B], U8, align_bytes=64)
 
         def flip(g, x_sb, copy_out):
-            flipped = psum.tile([P, 2, B], F32, name="flipped%d" % g)
+            flipped = psum.tile([P, 2, B], F32, name="flipped%d" % g, tag="rows%d" % g)
             for t in tiles:
                 words = x_sb[:, t, :].bitcast(F32)
                 for u in range(2):
@@ -130,43 +131,25 @@ def tile_bag_lstm_pb_s_kernel(
                 out=x_codes[:, g, :].bitcast(FP8X4), scales=x_scales[:, g, :], in_=grouped[:]
             )
 
-        def mx_pass(acc, t, g, w, start, stop):
-            rows = slice(t * P, (t + 1) * P)
+        def mx_pass(out, w, c, g, cols, start, stop):
             nc.tensor.matmul_mx(
-                out=acc[:],
-                lhsT=x_codes[:, g, rows].bitcast(FP8X4),
-                lhsT_scale=x_scales[:, g, rows],
-                rhs=w_words[:, w, :].bitcast(FP4X4),
-                rhs_scale=w_scales[:, w, :],
+                out=out,
+                lhsT=w_words[:, w, 2 * c * P : 2 * (c + 1) * P].bitcast(FP4X4),
+                lhsT_scale=w_scales[:, w, c * P : (c + 1) * P],
+                rhs=x_codes[:, g, cols].bitcast(FP8X4),
+                rhs_scale=x_scales[:, g, cols],
                 start=start,
                 stop=stop,
             )
 
-        gate_acc = [psum.tile([P, H], F32, name="gate_acc%d" % t) for t in tiles]
-        lin_acc = [psum.tile([P, H], F32, name="lin_acc%d" % t) for t in tiles]
-
+        squares = keep.tile([P, H], F32)
+        em_sq = per_row("em_sq")
+        nc.scalar.activation(out=squares[:], in_=main_sb[:, 0, :], func=ACT.Square, accum_out=col(em_sq, 0))
         main_grouped = flip(0, main_sb, nc.vector.tensor_copy)
         branch_grouped = flip(1, branch_sb, nc.scalar.copy)
 
-        bias_all = [keep.tile([P, H], F32, name="bias_all%d" % v) for v in range(2)]
-        for v in range(2):
-            spread_out = psum.tile([P, H], F32, name="spread_out%d" % v)
-            nc.tensor.matmul(out=spread_out[:], lhsT=ones[:], rhs=bias_rows[:, v, :], start=True, stop=True)
-            nc.scalar.copy(out=bias_all[v][:], in_=spread_out[:])
-
-        quantise(0, main_grouped)
-        quantise(1, branch_grouped)
-        for t in tiles:
-            mx_pass(gate_acc[t], t, 0, 0, True, False)
-            mx_pass(gate_acc[t], t, 1, 1, False, True)
-            mx_pass(lin_acc[t], t, 1, 2, True, True)
-
-        squares = keep.tile([P, H], F32)
-        em_sq = per_row("em_sq")
-        for t in tiles:
-            nc.scalar.activation(out=squares[:], in_=main_sb[:, t, :], func=ACT.Square, accum_out=col(em_sq, t))
-        em = per_row("em")
-        nc.gpsimd.tensor_tensor(out=em[:], in0=em_sq[:], in1=half[:], op=ALU.pow)
+        bias_ps = psum.tile([P, H], F32)
+        nc.tensor.matmul(out=bias_ps[:, 0 : 2 * CH_TILES], lhsT=bias_rows[:], rhs=pick[:], start=True, stop=True)
 
         bag = per_row("bag")
         nc.vector.tensor_copy(out=bag[:], in_=bag_bf[:])
@@ -174,21 +157,47 @@ def tile_bag_lstm_pb_s_kernel(
         nc.vector.tensor_scalar(
             out=one_minus_bag[:], in0=bag[:], scalar1=-1.0, scalar2=1.0, op0=ALU.mult, op1=ALU.add
         )
-        kept = big("kept")
-        for t in tiles:
-            nc.scalar.activation(out=kept[t][:], in_=main_sb[:, t, :], func=ACT.Copy, scale=col(one_minus_bag, t))
+        quantise(0, main_grouped)
+        bias_cols = keep.tile([P, 2 * CH_TILES], F32)
+        nc.vector.tensor_copy(out=bias_cols[:], in_=bias_ps[:, 0 : 2 * CH_TILES])
+        quantise(1, branch_grouped)
 
-        gate_b = big("gate_b")
-        lin_b = big("lin_b")
-        h_m = big("h_m")
+        acc = [psum.tile([P, 2, B], F32, name="acc%d" % c) for c in range(CH_TILES)]
+        for c in range(CH_TILES):
+            for t in tiles:
+                rows = slice(t * P, (t + 1) * P)
+                mx_pass(acc[c][:, 0, rows], 0, c, 0, rows, True, False)
+                mx_pass(acc[c][:, 0, rows], 1, c, 1, rows, False, True)
+            mx_pass(acc[c][:, 1, :], 2, c, 1, slice(0, B), True, True)
+
+        nc.scalar.activation(out=squares[:], in_=main_sb[:, 1, :], func=ACT.Square, accum_out=col(em_sq, 1))
+        em = per_row("em")
+        nc.gpsimd.tensor_tensor(out=em[:], in0=em_sq[:], in1=half[:], op=ALU.pow)
+        kept = big("kept")
+        nc.scalar.activation(out=kept[0][:], in_=main_sb[:, 0, :], func=ACT.Copy, scale=col(one_minus_bag, 0))
+
+        open_gate = keep.tile([P, CH_TILES, B], F32)
+        h_cols = keep.tile([P, CH_TILES, B], F32)
+        for c in range(CH_TILES):
+            nc.scalar.activation(
+                out=open_gate[:, c, :], in_=acc[c][:, 0, :], func=ACT.Relu, bias=bias_cols[:, c : c + 1]
+            )
+            nc.vector.scalar_tensor_tensor(
+                out=h_cols[:, c, :],
+                in0=acc[c][:, 1, :],
+                scalar=bias_cols[:, CH_TILES + c : CH_TILES + c + 1],
+                in1=open_gate[:, c, :],
+                op0=ALU.add,
+                op1=ALU.mult,
+            )
+        nc.scalar.activation(out=kept[1][:], in_=main_sb[:, 1, :], func=ACT.Copy, scale=col(one_minus_bag, 1))
+        h_m = [psum.tile([P, H], F32, name="h_m%d" % t, tag="rows%d" % t) for t in tiles]
+        for c in range(CH_TILES):
+            for t in tiles:
+                nc.tensor.transpose(h_m[t][:, c * P : (c + 1) * P], h_cols[:, c, t * P : (t + 1) * P], ident[:])
         hm_sq = per_row("hm_sq")
         gain = big("gain")
         for t in tiles:
-            nc.vector.tensor_tensor(out=gate_b[t][:], in0=gate_acc[t][:], in1=bias_all[0][:], op=ALU.add)
-            nc.vector.tensor_tensor(out=lin_b[t][:], in0=lin_acc[t][:], in1=bias_all[1][:], op=ALU.add)
-            nc.vector.scalar_tensor_tensor(
-                out=h_m[t][:], in0=gate_b[t][:], scalar=0.0, in1=lin_b[t][:], op0=ALU.max, op1=ALU.mult
-            )
             nc.scalar.activation(out=squares[:], in_=h_m[t][:], func=ACT.Square, accum_out=col(hm_sq, t))
         hm = per_row("hm")
         nc.gpsimd.tensor_tensor(out=hm[:], in0=hm_sq[:], in1=half[:], op=ALU.pow)

@@ -19,6 +19,8 @@ H = 512
 ROW_TILES = B // P
 CH_TILES = H // P
 WORDS = H // 2
+SPINS_BEFORE = 5
+SPINS_BETWEEN = 3
 LN_EPS = 1e-5
 BAG_EPS = 1e-6
 
@@ -62,12 +64,27 @@ def tile_bag_lstm_pb_s_kernel(
         def per_row(name):
             return keep.tile([P, ROW_TILES], F32, name=name)
 
+        still = keep.tile([P, 2 * P], F32)
+        nc.vector.memset(still[:], 0.0)
+        spin_ps = psum.tile([P, H], F32)
+
+        def spin(times):
+            for i in range(times):
+                nc.tensor.matmul(
+                    out=spin_ps[:, 0:P], lhsT=still[:, 0:P], rhs=still[:, P : 2 * P], start=True, stop=True
+                )
+
+        spin(SPINS_BEFORE)
+
         main_sb = keep.tile([P, ROW_TILES, H], BF16)
         nc.sync.dma_start(out=main_sb[:], in_=by_row_tile(main))
         branch_sb = keep.tile([P, ROW_TILES, H], BF16)
         nc.sync.dma_start(out=branch_sb[:], in_=by_row_tile(branch))
-        bag_bf = keep.tile([P, ROW_TILES], BF16)
-        nc.sync.dma_start(out=bag_bf[:], in_=is_bag.rearrange("(p t) one -> p (t one)", t=ROW_TILES))
+
+        bias_rows = [keep.tile([P, P], BF16, name="bias_rows%d" % v) for v in range(2)]
+        for v in range(2):
+            nc.vector.memset(bias_rows[v][:].bitcast(I32), 0)
+        nc.scalar.dma_start(out=bias_rows[0][0:CH_TILES, :], in_=b_mb.rearrange("(c p) -> c p", p=P))
 
         w_words = keep.tile([P, 3, 2 * H], U8, align_bytes=64)
         w_scales = keep.tile([P, 3, H], U8, align_bytes=64)
@@ -86,13 +103,12 @@ def tile_bag_lstm_pb_s_kernel(
             nc.sync.dma_start(
                 out=w_scales[r:P:32, 2, :].bitcast(I32), in_=W_b_scales[0, r:16:4, :].bitcast(I32)
             )
+        nc.sync.dma_start(out=bias_rows[1][0:CH_TILES, :], in_=b_b.rearrange("(c p) -> c p", p=P))
 
-        bias_rows = keep.tile([P, P], BF16)
-        nc.vector.memset(bias_rows[:].bitcast(I32), 0)
-        nc.gpsimd.dma_start(out=bias_rows[0:CH_TILES, :], in_=b_mb.rearrange("(c p) -> c p", p=P))
-        nc.gpsimd.dma_start(out=bias_rows[CH_TILES : 2 * CH_TILES, :], in_=b_b.rearrange("(c p) -> c p", p=P))
         ident = keep.tile([P, P], F32)
         make_identity(nc, ident[:])
+        bag_bf = keep.tile([P, ROW_TILES], BF16)
+        nc.gpsimd.dma_start(out=bag_bf[:], in_=is_bag.rearrange("(p t) one -> p (t one)", t=ROW_TILES))
         ln_b_all = keep.tile([P, H], BF16)
         nc.gpsimd.dma_start(out=ln_b_all[:], in_=ln_b.partition_broadcast(P))
         ln_g_all = keep.tile([P, H], BF16)
@@ -103,8 +119,8 @@ def tile_bag_lstm_pb_s_kernel(
         warm = keep.tile([P, 1], F32)
         nc.vector.memset(warm[:], 0.0)
         nc.scalar.activation(out=warm[:], in_=warm[:], func=ACT.Tanh)
-        pick = keep.tile([P, 2 * CH_TILES], BF16)
-        nc.vector.tensor_copy(out=pick[:], in_=ident[:, 0 : 2 * CH_TILES])
+        pick = keep.tile([P, CH_TILES], BF16)
+        nc.vector.tensor_copy(out=pick[:], in_=ident[:, 0:CH_TILES])
         half = per_row("half")
         nc.gpsimd.memset(half[:], 0.5)
         neg_half = per_row("neg_half")
@@ -144,12 +160,38 @@ def tile_bag_lstm_pb_s_kernel(
 
         squares = keep.tile([P, H], F32)
         em_sq = per_row("em_sq")
-        nc.scalar.activation(out=squares[:], in_=main_sb[:, 0, :], func=ACT.Square, accum_out=col(em_sq, 0))
+        for t in tiles:
+            nc.scalar.activation(out=squares[:], in_=main_sb[:, t, :], func=ACT.Square, accum_out=col(em_sq, t))
+        em = per_row("em")
+        nc.gpsimd.tensor_tensor(out=em[:], in0=em_sq[:], in1=half[:], op=ALU.pow)
+
         main_grouped = flip(0, main_sb, nc.vector.tensor_copy)
         branch_grouped = flip(1, branch_sb, nc.scalar.copy)
 
         bias_ps = psum.tile([P, H], F32)
-        nc.tensor.matmul(out=bias_ps[:, 0 : 2 * CH_TILES], lhsT=bias_rows[:], rhs=pick[:], start=True, stop=True)
+        bias_cols = [keep.tile([P, CH_TILES], F32, name="bias_cols%d" % v) for v in range(2)]
+
+        def bias_to_columns(v):
+            spot = bias_ps[:, v * CH_TILES : (v + 1) * CH_TILES]
+            nc.tensor.matmul(out=spot, lhsT=bias_rows[v][:], rhs=pick[:], start=True, stop=True)
+            nc.vector.tensor_copy(out=bias_cols[v][:], in_=spot)
+
+        quantise(0, main_grouped)
+        bias_to_columns(0)
+        quantise(1, branch_grouped)
+        spin(SPINS_BETWEEN)
+
+        acc = [psum.tile([P, 2, B], F32, name="acc%d" % c) for c in range(CH_TILES)]
+        open_gate = keep.tile([P, CH_TILES, B], F32)
+        h_cols = keep.tile([P, CH_TILES, B], F32)
+        for c in range(CH_TILES):
+            for t in tiles:
+                rows = slice(t * P, (t + 1) * P)
+                mx_pass(acc[c][:, 0, rows], 0, c, 0, rows, True, False)
+                mx_pass(acc[c][:, 0, rows], 1, c, 1, rows, False, True)
+            nc.scalar.activation(
+                out=open_gate[:, c, :], in_=acc[c][:, 0, :], func=ACT.Relu, bias=bias_cols[0][:, c : c + 1]
+            )
 
         bag = per_row("bag")
         nc.vector.tensor_copy(out=bag[:], in_=bag_bf[:])
@@ -157,40 +199,22 @@ def tile_bag_lstm_pb_s_kernel(
         nc.vector.tensor_scalar(
             out=one_minus_bag[:], in0=bag[:], scalar1=-1.0, scalar2=1.0, op0=ALU.mult, op1=ALU.add
         )
-        quantise(0, main_grouped)
-        bias_cols = keep.tile([P, 2 * CH_TILES], F32)
-        nc.vector.tensor_copy(out=bias_cols[:], in_=bias_ps[:, 0 : 2 * CH_TILES])
-        quantise(1, branch_grouped)
-
-        acc = [psum.tile([P, 2, B], F32, name="acc%d" % c) for c in range(CH_TILES)]
-        for c in range(CH_TILES):
-            for t in tiles:
-                rows = slice(t * P, (t + 1) * P)
-                mx_pass(acc[c][:, 0, rows], 0, c, 0, rows, True, False)
-                mx_pass(acc[c][:, 0, rows], 1, c, 1, rows, False, True)
-            mx_pass(acc[c][:, 1, :], 2, c, 1, slice(0, B), True, True)
-
-        nc.scalar.activation(out=squares[:], in_=main_sb[:, 1, :], func=ACT.Square, accum_out=col(em_sq, 1))
-        em = per_row("em")
-        nc.gpsimd.tensor_tensor(out=em[:], in0=em_sq[:], in1=half[:], op=ALU.pow)
         kept = big("kept")
-        nc.scalar.activation(out=kept[0][:], in_=main_sb[:, 0, :], func=ACT.Copy, scale=col(one_minus_bag, 0))
+        for t in tiles:
+            nc.vector.tensor_scalar_mul(out=kept[t][:], in0=main_sb[:, t, :], scalar1=col(one_minus_bag, t))
 
-        open_gate = keep.tile([P, CH_TILES, B], F32)
-        h_cols = keep.tile([P, CH_TILES, B], F32)
+        bias_to_columns(1)
         for c in range(CH_TILES):
-            nc.scalar.activation(
-                out=open_gate[:, c, :], in_=acc[c][:, 0, :], func=ACT.Relu, bias=bias_cols[:, c : c + 1]
-            )
+            mx_pass(acc[c][:, 1, :], 2, c, 1, slice(0, B), True, True)
             nc.vector.scalar_tensor_tensor(
                 out=h_cols[:, c, :],
                 in0=acc[c][:, 1, :],
-                scalar=bias_cols[:, CH_TILES + c : CH_TILES + c + 1],
+                scalar=bias_cols[1][:, c : c + 1],
                 in1=open_gate[:, c, :],
                 op0=ALU.add,
                 op1=ALU.mult,
             )
-        nc.scalar.activation(out=kept[1][:], in_=main_sb[:, 1, :], func=ACT.Copy, scale=col(one_minus_bag, 1))
+
         h_m = [psum.tile([P, H], F32, name="h_m%d" % t, tag="rows%d" % t) for t in tiles]
         for c in range(CH_TILES):
             for t in tiles:

@@ -66,7 +66,7 @@ def tile_bag_lstm_pb_s_kernel(
 
         still = keep.tile([P, 2 * P], F32)
         nc.vector.memset(still[:], 0.0)
-        spin_ps = psum.tile([P, H], F32)
+        spin_ps = psum.tile([P, H], F32, tag="spare0")
 
         def spin(times):
             for i in range(times):
@@ -104,23 +104,21 @@ def tile_bag_lstm_pb_s_kernel(
                 out=w_scales[r:P:32, 2, :].bitcast(I32), in_=W_b_scales[0, r:16:4, :].bitcast(I32)
             )
         nc.sync.dma_start(out=bias_rows[1][0:CH_TILES, :], in_=b_b.rearrange("(c p) -> c p", p=P))
+        ln_rows = keep.tile([P, P], BF16)
+        nc.vector.memset(ln_rows[:].bitcast(I32), 0)
+        nc.sync.dma_start(out=ln_rows[0:CH_TILES, :], in_=ln_g.rearrange("(c p) -> c p", p=P))
+        nc.sync.dma_start(out=ln_rows[CH_TILES : 2 * CH_TILES, :], in_=ln_b.rearrange("(c p) -> c p", p=P))
 
         ident = keep.tile([P, P], F32)
         make_identity(nc, ident[:])
         bag_bf = keep.tile([P, ROW_TILES], BF16)
         nc.gpsimd.dma_start(out=bag_bf[:], in_=is_bag.rearrange("(p t) one -> p (t one)", t=ROW_TILES))
-        ln_b_all = keep.tile([P, H], BF16)
-        nc.gpsimd.dma_start(out=ln_b_all[:], in_=ln_b.partition_broadcast(P))
-        ln_g_all = keep.tile([P, H], BF16)
-        nc.gpsimd.dma_start(out=ln_g_all[:], in_=ln_g.partition_broadcast(P))
-        o_sb = keep.tile([P, ROW_TILES, H], BF16)
-        nc.gpsimd.dma_start(out=o_sb[:], in_=by_row_tile(o))
 
         warm = keep.tile([P, 1], F32)
         nc.vector.memset(warm[:], 0.0)
         nc.scalar.activation(out=warm[:], in_=warm[:], func=ACT.Tanh)
-        pick = keep.tile([P, CH_TILES], BF16)
-        nc.vector.tensor_copy(out=pick[:], in_=ident[:, 0:CH_TILES])
+        pick = keep.tile([P, 2 * CH_TILES], BF16)
+        nc.vector.tensor_copy(out=pick[:], in_=ident[:, 0 : 2 * CH_TILES])
         half = per_row("half")
         nc.gpsimd.memset(half[:], 0.5)
         neg_half = per_row("neg_half")
@@ -164,16 +162,19 @@ def tile_bag_lstm_pb_s_kernel(
             nc.scalar.activation(out=squares[:], in_=main_sb[:, t, :], func=ACT.Square, accum_out=col(em_sq, t))
         em = per_row("em")
         nc.gpsimd.tensor_tensor(out=em[:], in0=em_sq[:], in1=half[:], op=ALU.pow)
+        o_sb = keep.tile([P, ROW_TILES, H], BF16)
+        nc.gpsimd.dma_start(out=o_sb[:], in_=by_row_tile(o))
 
         main_grouped = flip(0, main_sb, nc.vector.tensor_copy)
         branch_grouped = flip(1, branch_sb, nc.scalar.copy)
 
-        bias_ps = psum.tile([P, H], F32)
+        bias_ps = psum.tile([P, H], F32, tag="spare1")
         bias_cols = [keep.tile([P, CH_TILES], F32, name="bias_cols%d" % v) for v in range(2)]
+        ln_cols = keep.tile([P, 2 * CH_TILES], F32)
 
         def bias_to_columns(v):
             spot = bias_ps[:, v * CH_TILES : (v + 1) * CH_TILES]
-            nc.tensor.matmul(out=spot, lhsT=bias_rows[v][:], rhs=pick[:], start=True, stop=True)
+            nc.tensor.matmul(out=spot, lhsT=bias_rows[v][:], rhs=pick[:, 0:CH_TILES], start=True, stop=True)
             nc.vector.tensor_copy(out=bias_cols[v][:], in_=spot)
 
         quantise(0, main_grouped)
@@ -204,6 +205,9 @@ def tile_bag_lstm_pb_s_kernel(
             nc.vector.tensor_scalar_mul(out=kept[t][:], in0=main_sb[:, t, :], scalar1=col(one_minus_bag, t))
 
         bias_to_columns(1)
+        ln_spot = bias_ps[:, 2 * CH_TILES : 4 * CH_TILES]
+        nc.tensor.matmul(out=ln_spot, lhsT=ln_rows[:], rhs=pick[:], start=True, stop=True)
+        nc.vector.tensor_copy(out=ln_cols[:], in_=ln_spot)
         for c in range(CH_TILES):
             mx_pass(acc[c][:, 1, :], 2, c, 1, slice(0, B), True, True)
             nc.vector.scalar_tensor_tensor(
@@ -216,9 +220,23 @@ def tile_bag_lstm_pb_s_kernel(
             )
 
         h_m = [psum.tile([P, H], F32, name="h_m%d" % t, tag="rows%d" % t) for t in tiles]
-        for c in range(CH_TILES):
+
+        def back_to_rows(c):
             for t in tiles:
                 nc.tensor.transpose(h_m[t][:, c * P : (c + 1) * P], h_cols[:, c, t * P : (t + 1) * P], ident[:])
+
+        def repeat_on_all_partitions(first_col, spare):
+            repeated = psum.tile([P, H], F32, name="repeated%d" % spare, tag="spare%d" % spare)
+            for c in range(CH_TILES):
+                column = ln_cols[:, first_col + c : first_col + c + 1]
+                nc.tensor.transpose(repeated[:, c * P : (c + 1) * P], column.to_broadcast([P, P]), ident[:])
+            return repeated
+
+        ln_b_all = repeat_on_all_partitions(CH_TILES, 0)
+        back_to_rows(0)
+        ln_g_all = repeat_on_all_partitions(0, 1)
+        for c in range(1, CH_TILES):
+            back_to_rows(c)
         hm_sq = per_row("hm_sq")
         gain = big("gain")
         for t in tiles:

@@ -123,6 +123,8 @@ def tile_bag_lstm_pb_s_kernel(
         nc.gpsimd.memset(half[:], 0.5)
         neg_half = per_row("neg_half")
         nc.gpsimd.memset(neg_half[:], -0.5)
+        minus_one_hth = keep.tile([P, 1], F32)
+        nc.gpsimd.memset(minus_one_hth[:], -1.0 / H)
 
         x_codes = keep.tile([P, 2, B], U32, align_bytes=64)
         x_scales = keep.tile([P, 2, B], U8, align_bytes=64)
@@ -167,6 +169,11 @@ def tile_bag_lstm_pb_s_kernel(
 
         main_grouped = flip(0, main_sb, nc.vector.tensor_copy)
         branch_grouped = flip(1, branch_sb, nc.scalar.copy)
+        neg_mean_main = per_row("neg_mean_main")
+        for t in tiles:
+            nc.scalar.activation(
+                out=squares[:], in_=main_sb[:, t, :], func=ACT.Copy, scale=-1.0 / H, accum_out=col(neg_mean_main, t)
+            )
 
         bias_ps = psum.tile([P, H], F32, tag="spare1")
         bias_cols = [keep.tile([P, CH_TILES], F32, name="bias_cols%d" % v) for v in range(2)]
@@ -182,7 +189,7 @@ def tile_bag_lstm_pb_s_kernel(
         quantise(1, branch_grouped)
         spin(SPINS_BETWEEN)
 
-        acc = [psum.tile([P, 2, B], F32, name="acc%d" % c) for c in range(CH_TILES)]
+        acc = [psum.tile([P, 2, B], F32, name="acc%d" % c, tag="acc%d" % c) for c in range(CH_TILES)]
         open_gate = keep.tile([P, CH_TILES, B], F32)
         h_cols = keep.tile([P, CH_TILES, B], F32)
         for c in range(CH_TILES):
@@ -205,9 +212,6 @@ def tile_bag_lstm_pb_s_kernel(
             nc.vector.tensor_scalar_mul(out=kept[t][:], in0=main_sb[:, t, :], scalar1=col(one_minus_bag, t))
 
         bias_to_columns(1)
-        ln_spot = bias_ps[:, 2 * CH_TILES : 4 * CH_TILES]
-        nc.tensor.matmul(out=ln_spot, lhsT=ln_rows[:], rhs=pick[:], start=True, stop=True)
-        nc.vector.tensor_copy(out=ln_cols[:], in_=ln_spot)
         for c in range(CH_TILES):
             mx_pass(acc[c][:, 1, :], 2, c, 1, slice(0, B), True, True)
             nc.vector.scalar_tensor_tensor(
@@ -232,11 +236,23 @@ def tile_bag_lstm_pb_s_kernel(
                 nc.tensor.transpose(repeated[:, c * P : (c + 1) * P], column.to_broadcast([P, P]), ident[:])
             return repeated
 
-        ln_b_all = repeat_on_all_partitions(CH_TILES, 0)
-        back_to_rows(0)
-        ln_g_all = repeat_on_all_partitions(0, 1)
-        for c in range(1, CH_TILES):
+        for c in range(CH_TILES):
             back_to_rows(c)
+        ln_spot = bias_ps[:, 2 * CH_TILES : 4 * CH_TILES]
+        nc.tensor.matmul(out=ln_spot, lhsT=ln_rows[:], rhs=pick[:], start=True, stop=True)
+        nc.scalar.copy(out=ln_cols[:], in_=ln_spot)
+        ln_b_all = repeat_on_all_partitions(CH_TILES, 0)
+        ln_g_all = repeat_on_all_partitions(0, 1)
+        neg_mean_h = psum.tile([P, H], F32, tag="acc0")
+        for t in tiles:
+            for c in range(CH_TILES):
+                nc.tensor.matmul(
+                    out=col(neg_mean_h, t),
+                    lhsT=h_cols[:, c, t * P : (t + 1) * P],
+                    rhs=minus_one_hth[:],
+                    start=(c == 0),
+                    stop=(c == CH_TILES - 1),
+                )
         hm_sq = per_row("hm_sq")
         gain = big("gain")
         for t in tiles:
@@ -260,20 +276,20 @@ def tile_bag_lstm_pb_s_kernel(
         nc.vector.tensor_tensor(out=alpha[:], in0=alpha[:], in1=em[:], op=ALU.mult)
 
         pre = big("pre")
-        pre_sum = per_row("pre_sum")
         neg_mu = per_row("neg_mu")
         dev_sq = per_row("dev_sq")
         for t in tiles:
-            nc.vector.scalar_tensor_tensor(
-                out=pre[t][:],
-                in0=h_m[t][:],
-                scalar=col(alpha, t),
-                in1=main_sb[:, t, :],
-                op0=ALU.mult,
-                op1=ALU.add,
-                accum_out=col(pre_sum, t),
+            nc.scalar.activation(
+                out=col(neg_mu, t),
+                in_=col(neg_mean_h, t),
+                func=ACT.Identity,
+                scale=col(alpha, t),
+                bias=col(neg_mean_main, t),
             )
-            nc.vector.tensor_scalar_mul(out=col(neg_mu, t), in0=col(pre_sum, t), scalar1=-1.0 / H)
+        for t in tiles:
+            nc.vector.scalar_tensor_tensor(
+                out=pre[t][:], in0=h_m[t][:], scalar=col(alpha, t), in1=main_sb[:, t, :], op0=ALU.mult, op1=ALU.add
+            )
             nc.scalar.activation(
                 out=squares[:], in_=pre[t][:], func=ACT.Square, bias=col(neg_mu, t), accum_out=col(dev_sq, t)
             )
@@ -283,20 +299,28 @@ def tile_bag_lstm_pb_s_kernel(
                 out=centred[t][:], in0=pre[t][:], scalar=col(neg_mu, t), in1=gain[t][:], op0=ALU.add, op1=ALU.mult
             )
         rstd = per_row("rstd")
-        nc.vector.tensor_scalar(
-            out=rstd[:], in0=dev_sq[:], scalar1=1.0 / H, scalar2=LN_EPS, op0=ALU.mult, op1=ALU.add
-        )
+        nc.scalar.activation(out=rstd[:], in_=dev_sq[:], func=ACT.Copy, scale=1.0 / H, bias=LN_EPS)
         nc.gpsimd.tensor_tensor(out=rstd[:], in0=rstd[:], in1=neg_half[:], op=ALU.pow)
 
         shift_c = big("shift_c")
         squashed = big("squashed")
         h_out = big("h_out")
+        halves = [slice(0, H // 2), slice(H // 2, H)]
         for t in tiles:
-            nc.vector.scalar_tensor_tensor(
-                out=shift_c[t][:], in0=centred[t][:], scalar=col(rstd, t), in1=rest[t][:], op0=ALU.mult, op1=ALU.add
-            )
-            nc.sync.dma_start(out=by_row_tile(out_1)[:, t, :], in_=shift_c[t][:])
-            nc.scalar.activation(out=squashed[t][:], in_=shift_c[t][:], func=ACT.Tanh)
+            for half_row in halves:
+                nc.vector.scalar_tensor_tensor(
+                    out=shift_c[t][:, half_row],
+                    in0=centred[t][:, half_row],
+                    scalar=col(rstd, t),
+                    in1=rest[t][:, half_row],
+                    op0=ALU.mult,
+                    op1=ALU.add,
+                )
+                nc.sync.dma_start(out=by_row_tile(out_1)[:, t, half_row], in_=shift_c[t][:, half_row])
+                nc.scalar.activation(out=squashed[t][:, half_row], in_=shift_c[t][:, half_row], func=ACT.Tanh)
         for t in tiles:
-            nc.vector.tensor_tensor(out=h_out[t][:], in0=squashed[t][:], in1=o_sb[:, t, :], op=ALU.mult)
-            nc.sync.dma_start(out=by_row_tile(out_0)[:, t, :], in_=h_out[t][:])
+            for half_row in halves:
+                nc.vector.tensor_tensor(
+                    out=h_out[t][:, half_row], in0=squashed[t][:, half_row], in1=o_sb[:, t, half_row], op=ALU.mult
+                )
+                nc.sync.dma_start(out=by_row_tile(out_0)[:, t, half_row], in_=h_out[t][:, half_row])

@@ -89,30 +89,30 @@ def tile_bag_lstm_pb_s_kernel(
         w_words = keep.tile([P, 3, 2 * H], U8, align_bytes=64)
         w_scales = keep.tile([P, 3, H], U8, align_bytes=64)
         nc.vector.memset(w_scales[:].rearrange("p w n -> p (w n)").bitcast(I32), 0)
-        nc.sync.dma_start(
-            out=w_words[:, 0:2, :].bitcast(I32),
-            in_=W_mb_words.rearrange("g p n -> p g n").bitcast(I32),
-        )
         for r in range(4):
             nc.sync.dma_start(
                 out=w_scales[r:P:32, 0:2, :].bitcast(I32),
                 in_=W_mb_scales[:, r:16:4, :].rearrange("g q n -> q g n").bitcast(I32),
             )
+        nc.sync.dma_start(
+            out=w_words[:, 0:2, :].bitcast(I32),
+            in_=W_mb_words.rearrange("g p n -> p g n").bitcast(I32),
+        )
         nc.sync.dma_start(out=w_words[:, 2, :].bitcast(I32), in_=W_b_words[0].bitcast(I32))
         for r in range(4):
             nc.sync.dma_start(
                 out=w_scales[r:P:32, 2, :].bitcast(I32), in_=W_b_scales[0, r:16:4, :].bitcast(I32)
             )
         nc.sync.dma_start(out=bias_rows[1][0:CH_TILES, :], in_=b_b.rearrange("(c p) -> c p", p=P))
-        ln_rows = keep.tile([P, P], BF16)
-        nc.vector.memset(ln_rows[:].bitcast(I32), 0)
-        nc.sync.dma_start(out=ln_rows[0:CH_TILES, :], in_=ln_g.rearrange("(c p) -> c p", p=P))
-        nc.sync.dma_start(out=ln_rows[CH_TILES : 2 * CH_TILES, :], in_=ln_b.rearrange("(c p) -> c p", p=P))
 
         ident = keep.tile([P, P], F32)
         make_identity(nc, ident[:])
         bag_bf = keep.tile([P, ROW_TILES], BF16)
         nc.gpsimd.dma_start(out=bag_bf[:], in_=is_bag.rearrange("(p t) one -> p (t one)", t=ROW_TILES))
+        ln_rows = keep.tile([P, P], BF16)
+        nc.vector.memset(ln_rows[:].bitcast(I32), 0)
+        nc.gpsimd.dma_start(out=ln_rows[0:CH_TILES, :], in_=ln_g.rearrange("(c p) -> c p", p=P))
+        nc.gpsimd.dma_start(out=ln_rows[CH_TILES : 2 * CH_TILES, :], in_=ln_b.rearrange("(c p) -> c p", p=P))
 
         warm = keep.tile([P, 1], F32)
         nc.vector.memset(warm[:], 0.0)
@@ -236,13 +236,15 @@ def tile_bag_lstm_pb_s_kernel(
                 nc.tensor.transpose(repeated[:, c * P : (c + 1) * P], column.to_broadcast([P, P]), ident[:])
             return repeated
 
-        for c in range(CH_TILES):
-            back_to_rows(c)
         ln_spot = bias_ps[:, 2 * CH_TILES : 4 * CH_TILES]
         nc.tensor.matmul(out=ln_spot, lhsT=ln_rows[:], rhs=pick[:], start=True, stop=True)
         nc.scalar.copy(out=ln_cols[:], in_=ln_spot)
-        ln_b_all = repeat_on_all_partitions(CH_TILES, 0)
-        ln_g_all = repeat_on_all_partitions(0, 1)
+        back_to_rows(0)
+        back_to_rows(1)
+        ln_g_all = repeat_on_all_partitions(0, 0)
+        back_to_rows(2)
+        ln_b_all = repeat_on_all_partitions(CH_TILES, 1)
+        back_to_rows(3)
         neg_mean_h = psum.tile([P, H], F32, tag="acc0")
         for t in tiles:
             for c in range(CH_TILES):

@@ -245,16 +245,15 @@ def tile_bag_lstm_pb_s_kernel(
         back_to_rows(2)
         ln_b_all = repeat_on_all_partitions(CH_TILES, 1)
         back_to_rows(3)
-        neg_mean_h = psum.tile([P, H], F32, tag="acc0")
-        for t in tiles:
-            for c in range(CH_TILES):
-                nc.tensor.matmul(
-                    out=col(neg_mean_h, t),
-                    lhsT=h_cols[:, c, t * P : (t + 1) * P],
-                    rhs=minus_one_hth[:],
-                    start=(c == 0),
-                    stop=(c == CH_TILES - 1),
-                )
+        neg_mean_h0 = psum.tile([P, H], F32, tag="acc0")
+        for c in range(CH_TILES):
+            nc.tensor.matmul(
+                out=neg_mean_h0[:, 0:1],
+                lhsT=h_cols[:, c, 0:P],
+                rhs=minus_one_hth[:],
+                start=(c == 0),
+                stop=(c == CH_TILES - 1),
+            )
         hm_sq = per_row("hm_sq")
         gain = big("gain")
         for t in tiles:
@@ -269,6 +268,17 @@ def tile_bag_lstm_pb_s_kernel(
             nc.vector.scalar_tensor_tensor(
                 out=rest[t][:], in0=ln_b_all[:], scalar=col(bag, t), in1=kept[t][:], op0=ALU.mult, op1=ALU.add
             )
+        neg_mean_h1 = keep.tile([P, 1], F32)
+        scaled = keep.tile([P, H], F32)
+        nc.vector.tensor_scalar(
+            out=scaled[:],
+            in0=h_m[1][:],
+            scalar1=-1.0 / H,
+            scalar2=None,
+            op0=ALU.mult,
+            op1=ALU.add,
+            accum_out=neg_mean_h1[:],
+        )
 
         alpha = per_row("alpha")
         nc.vector.scalar_tensor_tensor(
@@ -280,14 +290,20 @@ def tile_bag_lstm_pb_s_kernel(
         pre = big("pre")
         neg_mu = per_row("neg_mu")
         dev_sq = per_row("dev_sq")
-        for t in tiles:
-            nc.scalar.activation(
-                out=col(neg_mu, t),
-                in_=col(neg_mean_h, t),
-                func=ACT.Identity,
-                scale=col(alpha, t),
-                bias=col(neg_mean_main, t),
-            )
+        nc.scalar.activation(
+            out=col(neg_mu, 0),
+            in_=neg_mean_h0[:, 0:1],
+            func=ACT.Identity,
+            scale=col(alpha, 0),
+            bias=col(neg_mean_main, 0),
+        )
+        nc.scalar.activation(
+            out=col(neg_mu, 1),
+            in_=neg_mean_h1[:],
+            func=ACT.Identity,
+            scale=col(alpha, 1),
+            bias=col(neg_mean_main, 1),
+        )
         for t in tiles:
             nc.vector.scalar_tensor_tensor(
                 out=pre[t][:], in0=h_m[t][:], scalar=col(alpha, t), in1=main_sb[:, t, :], op0=ALU.mult, op1=ALU.add

@@ -20,7 +20,7 @@ ROW_TILES = B // P
 CH_TILES = H // P
 WORDS = H // 2
 SPINS_BEFORE = 5
-SPINS_BETWEEN = 3
+SPINS_BETWEEN = 2
 LN_EPS = 1e-5
 BAG_EPS = 1e-6
 
@@ -129,22 +129,27 @@ def tile_bag_lstm_pb_s_kernel(
         x_codes = keep.tile([P, 2, B], U32, align_bytes=64)
         x_scales = keep.tile([P, 2, B], U8, align_bytes=64)
 
-        def flip(g, x_sb, copy_out):
-            flipped = psum.tile([P, 2, B], F32, name="flipped%d" % g, tag="rows%d" % g)
-            for t in tiles:
-                words = x_sb[:, t, :].bitcast(F32)
+        grouped = [keep.tile([P, 4 * B], BF16, align_bytes=64, name="grouped%d" % g) for g in range(2)]
+
+        def flip(g, x_sb, first, count, bank, copy_out):
+            flipped = psum.tile([P, 2, count * P], F32, name="flipped%d%d" % (g, first), tag=bank)
+            for i in range(count):
+                words = x_sb[:, first + i, :].bitcast(F32)
                 for u in range(2):
-                    nc.tensor.transpose(flipped[:, u, t * P : (t + 1) * P], words[:, u:WORDS:2], ident[:])
-            grouped = keep.tile([P, 4 * B], BF16, align_bytes=64, name="grouped%d" % g)
+                    nc.tensor.transpose(flipped[:, u, i * P : (i + 1) * P], words[:, u:WORDS:2], ident[:])
             copy_out(
-                out=grouped[:].bitcast(F32).rearrange("p (c u) -> p c u", u=2),
+                out=grouped[g][:, 4 * first * P : 4 * (first + count) * P]
+                .bitcast(F32)
+                .rearrange("p (c u) -> p c u", u=2),
                 in_=flipped[:].rearrange("p u c -> p c u"),
             )
-            return grouped
 
-        def quantise(g, grouped):
+        def quantise(g, first, count):
+            rows = slice(first * P, (first + count) * P)
             nc.vector.quantize_mx(
-                out=x_codes[:, g, :].bitcast(FP8X4), scales=x_scales[:, g, :], in_=grouped[:]
+                out=x_codes[:, g, rows].bitcast(FP8X4),
+                scales=x_scales[:, g, rows],
+                in_=grouped[g][:, 4 * first * P : 4 * (first + count) * P],
             )
 
         def mx_pass(out, w, c, g, cols, start, stop):
@@ -167,8 +172,9 @@ def tile_bag_lstm_pb_s_kernel(
         o_sb = keep.tile([P, ROW_TILES, H], BF16)
         nc.gpsimd.dma_start(out=o_sb[:], in_=by_row_tile(o))
 
-        main_grouped = flip(0, main_sb, nc.vector.tensor_copy)
-        branch_grouped = flip(1, branch_sb, nc.scalar.copy)
+        flip(0, main_sb, 0, ROW_TILES, "rows0", nc.vector.tensor_copy)
+        flip(1, branch_sb, 0, 1, "rows1", nc.scalar.copy)
+        flip(1, branch_sb, 1, 1, "acc3", nc.scalar.copy)
         neg_mean_main = per_row("neg_mean_main")
         for t in tiles:
             nc.scalar.activation(
@@ -184,9 +190,10 @@ def tile_bag_lstm_pb_s_kernel(
             nc.tensor.matmul(out=spot, lhsT=bias_rows[v][:], rhs=pick[:, 0:CH_TILES], start=True, stop=True)
             nc.vector.tensor_copy(out=bias_cols[v][:], in_=spot)
 
-        quantise(0, main_grouped)
+        quantise(0, 0, ROW_TILES)
         bias_to_columns(0)
-        quantise(1, branch_grouped)
+        quantise(1, 0, 1)
+        quantise(1, 1, 1)
         spin(SPINS_BETWEEN)
 
         acc = [psum.tile([P, 2, B], F32, name="acc%d" % c, tag="acc%d" % c) for c in range(CH_TILES)]
@@ -304,6 +311,7 @@ def tile_bag_lstm_pb_s_kernel(
             scale=col(alpha, 1),
             bias=col(neg_mean_main, 1),
         )
+        rstd = per_row("rstd")
         for t in tiles:
             nc.vector.scalar_tensor_tensor(
                 out=pre[t][:], in0=h_m[t][:], scalar=col(alpha, t), in1=main_sb[:, t, :], op0=ALU.mult, op1=ALU.add
@@ -311,14 +319,13 @@ def tile_bag_lstm_pb_s_kernel(
             nc.scalar.activation(
                 out=squares[:], in_=pre[t][:], func=ACT.Square, bias=col(neg_mu, t), accum_out=col(dev_sq, t)
             )
+            nc.scalar.activation(out=col(rstd, t), in_=col(dev_sq, t), func=ACT.Copy, scale=1.0 / H, bias=LN_EPS)
+            nc.gpsimd.tensor_tensor(out=col(rstd, t), in0=col(rstd, t), in1=col(neg_half, t), op=ALU.pow)
         centred = big("centred")
         for t in tiles:
             nc.vector.scalar_tensor_tensor(
                 out=centred[t][:], in0=pre[t][:], scalar=col(neg_mu, t), in1=gain[t][:], op0=ALU.add, op1=ALU.mult
             )
-        rstd = per_row("rstd")
-        nc.scalar.activation(out=rstd[:], in_=dev_sq[:], func=ACT.Copy, scale=1.0 / H, bias=LN_EPS)
-        nc.gpsimd.tensor_tensor(out=rstd[:], in0=rstd[:], in1=neg_half[:], op=ALU.pow)
 
         shift_c = big("shift_c")
         squashed = big("squashed")

@@ -23,6 +23,7 @@ SPINS_BEFORE = 5
 SPINS_BETWEEN = 2
 LN_EPS = 1e-5
 BAG_EPS = 1e-6
+EM_FLOOR = 1e-12
 
 FLOPS = 2 * B * (2 * H) * H + 2 * B * H * H
 
@@ -66,7 +67,7 @@ def tile_bag_lstm_pb_s_kernel(
 
         still = keep.tile([P, 2 * P], F32)
         nc.vector.memset(still[:], 0.0)
-        spin_ps = psum.tile([P, H], F32, tag="spare0")
+        spin_ps = psum.tile([P, H], F32, tag="bank3")
 
         def spin(times):
             for i in range(times):
@@ -84,7 +85,7 @@ def tile_bag_lstm_pb_s_kernel(
         bias_rows = [keep.tile([P, P], BF16, name="bias_rows%d" % v) for v in range(2)]
         for v in range(2):
             nc.vector.memset(bias_rows[v][:].bitcast(I32), 0)
-        nc.scalar.dma_start(out=bias_rows[0][0:CH_TILES, :], in_=b_mb.rearrange("(c p) -> c p", p=P))
+        nc.sync.dma_start(out=bias_rows[0][0:CH_TILES, :], in_=b_mb.rearrange("(c p) -> c p", p=P))
 
         w_words = keep.tile([P, 3, 2 * H], U8, align_bytes=64)
         w_scales = keep.tile([P, 3, H], U8, align_bytes=64)
@@ -104,11 +105,11 @@ def tile_bag_lstm_pb_s_kernel(
                 out=w_scales[r:P:32, 2, :].bitcast(I32), in_=W_b_scales[0, r:16:4, :].bitcast(I32)
             )
         nc.sync.dma_start(out=bias_rows[1][0:CH_TILES, :], in_=b_b.rearrange("(c p) -> c p", p=P))
+        bag = keep.tile([P, ROW_TILES], BF16)
+        nc.sync.dma_start(out=bag[:], in_=is_bag.rearrange("(p t) one -> p (t one)", t=ROW_TILES))
 
         ident = keep.tile([P, P], F32)
         make_identity(nc, ident[:])
-        bag_bf = keep.tile([P, ROW_TILES], BF16)
-        nc.gpsimd.dma_start(out=bag_bf[:], in_=is_bag.rearrange("(p t) one -> p (t one)", t=ROW_TILES))
         ln_rows = keep.tile([P, P], BF16)
         nc.vector.memset(ln_rows[:].bitcast(I32), 0)
         nc.gpsimd.dma_start(out=ln_rows[0:CH_TILES, :], in_=ln_g.rearrange("(c p) -> c p", p=P))
@@ -123,8 +124,6 @@ def tile_bag_lstm_pb_s_kernel(
         nc.gpsimd.memset(half[:], 0.5)
         neg_half = per_row("neg_half")
         nc.gpsimd.memset(neg_half[:], -0.5)
-        minus_one_hth = keep.tile([P, 1], F32)
-        nc.gpsimd.memset(minus_one_hth[:], -1.0 / H)
 
         x_codes = keep.tile([P, 2, B], U32, align_bytes=64)
         x_scales = keep.tile([P, 2, B], U8, align_bytes=64)
@@ -167,164 +166,163 @@ def tile_bag_lstm_pb_s_kernel(
         em_sq = per_row("em_sq")
         for t in tiles:
             nc.scalar.activation(out=squares[:], in_=main_sb[:, t, :], func=ACT.Square, accum_out=col(em_sq, t))
-        em = per_row("em")
-        nc.gpsimd.tensor_tensor(out=em[:], in0=em_sq[:], in1=half[:], op=ALU.pow)
+        inv_em = per_row("inv_em")
+        nc.gpsimd.tensor_scalar(
+            out=em_sq[:], in0=em_sq[:], scalar1=EM_FLOOR * EM_FLOOR, scalar2=None, op0=ALU.max
+        )
+        nc.gpsimd.tensor_tensor(out=inv_em[:], in0=em_sq[:], in1=neg_half[:], op=ALU.pow)
+        eps_over_em = per_row("eps_over_em")
+        nc.gpsimd.tensor_scalar(
+            out=eps_over_em[:], in0=inv_em[:], scalar1=BAG_EPS, scalar2=0.0, op0=ALU.mult, op1=ALU.add
+        )
         o_sb = keep.tile([P, ROW_TILES, H], BF16)
         nc.gpsimd.dma_start(out=o_sb[:], in_=by_row_tile(o))
-
-        flip(0, main_sb, 0, ROW_TILES, "rows0", nc.vector.tensor_copy)
-        flip(1, branch_sb, 0, 1, "rows1", nc.scalar.copy)
-        flip(1, branch_sb, 1, 1, "acc3", nc.scalar.copy)
-        neg_mean_main = per_row("neg_mean_main")
+        one_minus_bag = per_row("one_minus_bag")
+        nc.gpsimd.tensor_scalar(
+            out=one_minus_bag[:], in0=bag[:], scalar1=-1.0, scalar2=1.0, op0=ALU.mult, op1=ALU.add
+        )
+        kept = big("kept")
         for t in tiles:
-            nc.scalar.activation(
-                out=squares[:], in_=main_sb[:, t, :], func=ACT.Copy, scale=-1.0 / H, accum_out=col(neg_mean_main, t)
+            nc.gpsimd.tensor_scalar(
+                out=kept[t][:], in0=main_sb[:, t, :], scalar1=col(one_minus_bag, t), scalar2=0.0, op0=ALU.mult, op1=ALU.add
             )
 
-        bias_ps = psum.tile([P, H], F32, tag="spare1")
+        flip(0, main_sb, 0, ROW_TILES, "bank4", nc.vector.tensor_copy)
+        flip(1, branch_sb, 0, 1, "bank5", nc.scalar.copy)
+        flip(1, branch_sb, 1, 1, "bank6", nc.scalar.copy)
+
+        bias_ps = psum.tile([P, H], F32, tag="bank7")
         bias_cols = [keep.tile([P, CH_TILES], F32, name="bias_cols%d" % v) for v in range(2)]
-        ln_cols = keep.tile([P, 2 * CH_TILES], F32)
 
         def bias_to_columns(v):
             spot = bias_ps[:, v * CH_TILES : (v + 1) * CH_TILES]
             nc.tensor.matmul(out=spot, lhsT=bias_rows[v][:], rhs=pick[:, 0:CH_TILES], start=True, stop=True)
             nc.vector.tensor_copy(out=bias_cols[v][:], in_=spot)
 
-        quantise(0, 0, ROW_TILES)
-        bias_to_columns(0)
-        quantise(1, 0, 1)
-        quantise(1, 1, 1)
         spin(SPINS_BETWEEN)
+        for t in tiles:
+            quantise(0, t, 1)
+            quantise(1, t, 1)
+        bias_to_columns(0)
 
-        acc = [psum.tile([P, 2, B], F32, name="acc%d" % c, tag="acc%d" % c) for c in range(CH_TILES)]
+        gate = [psum.tile([P, B], F32, name="gate%d" % c, tag="bank%d" % (2 * c)) for c in range(CH_TILES)]
+        lin = [psum.tile([P, B], F32, name="lin%d" % c, tag="bank%d" % (2 * c + 1)) for c in range(CH_TILES)]
         open_gate = keep.tile([P, CH_TILES, B], F32)
         h_cols = keep.tile([P, CH_TILES, B], F32)
-        for c in range(CH_TILES):
-            for t in tiles:
-                rows = slice(t * P, (t + 1) * P)
-                mx_pass(acc[c][:, 0, rows], 0, c, 0, rows, True, False)
-                mx_pass(acc[c][:, 0, rows], 1, c, 1, rows, False, True)
+
+        def gate_passes(c, t):
+            rows = slice(t * P, (t + 1) * P)
+            mx_pass(gate[c][:, rows], 0, c, 0, rows, True, False)
+            mx_pass(gate[c][:, rows], 1, c, 1, rows, False, True)
+
+        def relu(c):
             nc.scalar.activation(
-                out=open_gate[:, c, :], in_=acc[c][:, 0, :], func=ACT.Relu, bias=bias_cols[0][:, c : c + 1]
+                out=open_gate[:, c, :], in_=gate[c][:], func=ACT.Relu, bias=bias_cols[0][:, c : c + 1]
             )
 
-        bag = per_row("bag")
-        nc.vector.tensor_copy(out=bag[:], in_=bag_bf[:])
-        one_minus_bag = per_row("one_minus_bag")
-        nc.vector.tensor_scalar(
-            out=one_minus_bag[:], in0=bag[:], scalar1=-1.0, scalar2=1.0, op0=ALU.mult, op1=ALU.add
-        )
-        kept = big("kept")
-        for t in tiles:
-            nc.vector.tensor_scalar_mul(out=kept[t][:], in0=main_sb[:, t, :], scalar1=col(one_minus_bag, t))
+        def lin_pass(c):
+            mx_pass(lin[c][:], 2, c, 1, slice(0, B), True, True)
 
-        bias_to_columns(1)
-        for c in range(CH_TILES):
-            mx_pass(acc[c][:, 1, :], 2, c, 1, slice(0, B), True, True)
+        def product(c):
             nc.vector.scalar_tensor_tensor(
                 out=h_cols[:, c, :],
-                in0=acc[c][:, 1, :],
+                in0=lin[c][:],
                 scalar=bias_cols[1][:, c : c + 1],
                 in1=open_gate[:, c, :],
                 op0=ALU.add,
                 op1=ALU.mult,
             )
 
-        h_m = [psum.tile([P, H], F32, name="h_m%d" % t, tag="rows%d" % t) for t in tiles]
+        for t in tiles:
+            for c in range(2):
+                gate_passes(c, t)
+        relu(0)
+        relu(1)
+        lin_pass(0)
+        lin_pass(1)
+        bias_to_columns(1)
+        product(0)
+        product(1)
+        ln_cols = keep.tile([P, 2 * CH_TILES], F32)
+        ln_ps = psum.tile([P, H], F32, tag="bank7")
+        nc.tensor.matmul(out=ln_ps[:, 0 : 2 * CH_TILES], lhsT=ln_rows[:], rhs=pick[:], start=True, stop=True)
+        nc.scalar.copy(out=ln_cols[:], in_=ln_ps[:, 0 : 2 * CH_TILES])
+        for c in range(2, CH_TILES):
+            for t in tiles:
+                gate_passes(c, t)
+            relu(c)
+            lin_pass(c)
+            product(c)
+
+        h_m = [psum.tile([P, H], F32, name="h_m%d" % t, tag="bank%d" % (2 * t)) for t in tiles]
 
         def back_to_rows(c):
             for t in tiles:
                 nc.tensor.transpose(h_m[t][:, c * P : (c + 1) * P], h_cols[:, c, t * P : (t + 1) * P], ident[:])
 
-        def repeat_on_all_partitions(first_col, spare):
-            repeated = psum.tile([P, H], F32, name="repeated%d" % spare, tag="spare%d" % spare)
+        def repeat_on_all_partitions(first_col, bank):
+            repeated = psum.tile([P, H], F32, name="repeated%d" % first_col, tag=bank)
             for c in range(CH_TILES):
                 column = ln_cols[:, first_col + c : first_col + c + 1]
                 nc.tensor.transpose(repeated[:, c * P : (c + 1) * P], column.to_broadcast([P, P]), ident[:])
             return repeated
 
-        ln_spot = bias_ps[:, 2 * CH_TILES : 4 * CH_TILES]
-        nc.tensor.matmul(out=ln_spot, lhsT=ln_rows[:], rhs=pick[:], start=True, stop=True)
-        nc.scalar.copy(out=ln_cols[:], in_=ln_spot)
-        back_to_rows(0)
-        back_to_rows(1)
-        ln_g_all = repeat_on_all_partitions(0, 0)
-        back_to_rows(2)
-        ln_b_all = repeat_on_all_partitions(CH_TILES, 1)
-        back_to_rows(3)
-        neg_mean_h0 = psum.tile([P, H], F32, tag="acc0")
+        ln_b_all = repeat_on_all_partitions(CH_TILES, "bank1")
         for c in range(CH_TILES):
-            nc.tensor.matmul(
-                out=neg_mean_h0[:, 0:1],
-                lhsT=h_cols[:, c, 0:P],
-                rhs=minus_one_hth[:],
-                start=(c == 0),
-                stop=(c == CH_TILES - 1),
+            back_to_rows(c)
+        ln_g_all = repeat_on_all_partitions(0, "bank3")
+
+        ratio_sq = per_row("ratio_sq")
+        ratio = per_row("ratio")
+        for t in tiles:
+            nc.scalar.activation(
+                out=squares[:], in_=h_m[t][:], func=ACT.Square, scale=col(inv_em, t), accum_out=col(ratio_sq, t)
             )
-        hm_sq = per_row("hm_sq")
-        gain = big("gain")
-        for t in tiles:
-            nc.scalar.activation(out=squares[:], in_=h_m[t][:], func=ACT.Square, accum_out=col(hm_sq, t))
-        hm = per_row("hm")
-        nc.gpsimd.tensor_tensor(out=hm[:], in0=hm_sq[:], in1=half[:], op=ALU.pow)
-        for t in tiles:
-            nc.scalar.activation(out=gain[t][:], in_=ln_g_all[:], func=ACT.Copy, scale=col(bag, t))
+            nc.gpsimd.tensor_tensor(out=col(ratio, t), in0=col(ratio_sq, t), in1=col(half, t), op=ALU.pow)
 
         rest = big("rest")
         for t in tiles:
             nc.vector.scalar_tensor_tensor(
                 out=rest[t][:], in0=ln_b_all[:], scalar=col(bag, t), in1=kept[t][:], op0=ALU.mult, op1=ALU.add
             )
-        neg_mean_h1 = keep.tile([P, 1], F32)
-        scaled = keep.tile([P, H], F32)
-        nc.vector.tensor_scalar(
-            out=scaled[:],
-            in0=h_m[1][:],
-            scalar1=-1.0 / H,
-            scalar2=None,
-            op0=ALU.mult,
-            op1=ALU.add,
-            accum_out=neg_mean_h1[:],
-        )
 
-        alpha = per_row("alpha")
-        nc.vector.scalar_tensor_tensor(
-            out=alpha[:], in0=hm[:], scalar=BAG_EPS, in1=em[:], op0=ALU.add, op1=ALU.max
-        )
-        nc.vector.reciprocal(out=alpha[:], in_=alpha[:])
-        nc.vector.tensor_tensor(out=alpha[:], in0=alpha[:], in1=em[:], op=ALU.mult)
-
+        stretch = per_row("stretch")
+        eps_row = per_row("eps_row")
         pre = big("pre")
-        neg_mu = per_row("neg_mu")
+        pre_sum = per_row("pre_sum")
+        mean = per_row("mean")
         dev_sq = per_row("dev_sq")
-        nc.scalar.activation(
-            out=col(neg_mu, 0),
-            in_=neg_mean_h0[:, 0:1],
-            func=ACT.Identity,
-            scale=col(alpha, 0),
-            bias=col(neg_mean_main, 0),
-        )
-        nc.scalar.activation(
-            out=col(neg_mu, 1),
-            in_=neg_mean_h1[:],
-            func=ACT.Identity,
-            scale=col(alpha, 1),
-            bias=col(neg_mean_main, 1),
-        )
-        rstd = per_row("rstd")
-        for t in tiles:
-            nc.vector.scalar_tensor_tensor(
-                out=pre[t][:], in0=h_m[t][:], scalar=col(alpha, t), in1=main_sb[:, t, :], op0=ALU.mult, op1=ALU.add
-            )
-            nc.scalar.activation(
-                out=squares[:], in_=pre[t][:], func=ACT.Square, bias=col(neg_mu, t), accum_out=col(dev_sq, t)
-            )
-            nc.scalar.activation(out=col(rstd, t), in_=col(dev_sq, t), func=ACT.Copy, scale=1.0 / H, bias=LN_EPS)
-            nc.gpsimd.tensor_tensor(out=col(rstd, t), in0=col(rstd, t), in1=col(neg_half, t), op=ALU.pow)
+        spread = per_row("spread")
+        factor = per_row("factor")
         centred = big("centred")
         for t in tiles:
+            nc.vector.tensor_scalar(
+                out=col(stretch, t), in0=col(ratio, t), scalar1=col(eps_over_em, t), scalar2=1.0, op0=ALU.add, op1=ALU.max
+            )
             nc.vector.scalar_tensor_tensor(
-                out=centred[t][:], in0=pre[t][:], scalar=col(neg_mu, t), in1=gain[t][:], op0=ALU.add, op1=ALU.mult
+                out=pre[t][:],
+                in0=main_sb[:, t, :],
+                scalar=col(stretch, t),
+                in1=h_m[t][:],
+                op0=ALU.mult,
+                op1=ALU.add,
+                accum_out=col(pre_sum, t),
+            )
+            nc.vector.scalar_tensor_tensor(
+                out=col(eps_row, t), in0=col(stretch, t), scalar=LN_EPS, in1=col(stretch, t), op0=ALU.mult, op1=ALU.mult
+            )
+            nc.scalar.activation(
+                out=squares[:], in_=pre[t][:], func=ACT.Square, scale=-1.0 * H, bias=col(pre_sum, t), accum_out=col(dev_sq, t)
+            )
+            nc.scalar.activation(
+                out=col(spread, t), in_=col(dev_sq, t), func=ACT.Identity, scale=1.0 / H / H / H, bias=col(eps_row, t)
+            )
+        nc.vector.tensor_scalar_mul(out=mean[:], in0=pre_sum[:], scalar1=1.0 / H)
+        for t in tiles:
+            nc.gpsimd.tensor_tensor(out=col(spread, t), in0=col(spread, t), in1=col(neg_half, t), op=ALU.pow)
+            nc.gpsimd.tensor_tensor(out=col(factor, t), in0=col(spread, t), in1=col(bag, t), op=ALU.mult)
+            nc.vector.scalar_tensor_tensor(
+                out=centred[t][:], in0=pre[t][:], scalar=col(mean, t), in1=ln_g_all[:], op0=ALU.subtract, op1=ALU.mult
             )
 
         shift_c = big("shift_c")
@@ -336,7 +334,7 @@ def tile_bag_lstm_pb_s_kernel(
                 nc.vector.scalar_tensor_tensor(
                     out=shift_c[t][:, half_row],
                     in0=centred[t][:, half_row],
-                    scalar=col(rstd, t),
+                    scalar=col(factor, t),
                     in1=rest[t][:, half_row],
                     op0=ALU.mult,
                     op1=ALU.add,

@@ -99,17 +99,17 @@ def tile_bag_lstm_pb_s_kernel(
             out=w_words[:, 0:2, :].bitcast(I32),
             in_=W_mb_words.rearrange("g p n -> p g n").bitcast(I32),
         )
+        nc.sync.dma_start(out=bias_rows[1][0:CH_TILES, :], in_=b_b.rearrange("(c p) -> c p", p=P))
         nc.sync.dma_start(out=w_words[:, 2, :].bitcast(I32), in_=W_b_words[0].bitcast(I32))
         for r in range(4):
             nc.sync.dma_start(
                 out=w_scales[r:P:32, 2, :].bitcast(I32), in_=W_b_scales[0, r:16:4, :].bitcast(I32)
             )
-        nc.sync.dma_start(out=bias_rows[1][0:CH_TILES, :], in_=b_b.rearrange("(c p) -> c p", p=P))
-        bag = keep.tile([P, ROW_TILES], BF16)
-        nc.sync.dma_start(out=bag[:], in_=is_bag.rearrange("(p t) one -> p (t one)", t=ROW_TILES))
 
         ident = keep.tile([P, P], F32)
         make_identity(nc, ident[:])
+        bag = keep.tile([P, ROW_TILES], BF16)
+        nc.gpsimd.dma_start(out=bag[:], in_=is_bag.rearrange("(p t) one -> p (t one)", t=ROW_TILES))
         ln_rows = keep.tile([P, P], BF16)
         nc.vector.memset(ln_rows[:].bitcast(I32), 0)
         nc.gpsimd.dma_start(out=ln_rows[0:CH_TILES, :], in_=ln_g.rearrange("(c p) -> c p", p=P))
@@ -177,25 +177,15 @@ def tile_bag_lstm_pb_s_kernel(
         )
         o_sb = keep.tile([P, ROW_TILES, H], BF16)
         nc.gpsimd.dma_start(out=o_sb[:], in_=by_row_tile(o))
-        one_minus_bag = per_row("one_minus_bag")
-        nc.gpsimd.tensor_scalar(
-            out=one_minus_bag[:], in0=bag[:], scalar1=-1.0, scalar2=1.0, op0=ALU.mult, op1=ALU.add
-        )
-        kept = big("kept")
-        for t in tiles:
-            nc.gpsimd.tensor_scalar(
-                out=kept[t][:], in0=main_sb[:, t, :], scalar1=col(one_minus_bag, t), scalar2=0.0, op0=ALU.mult, op1=ALU.add
-            )
-
         flip(0, main_sb, 0, ROW_TILES, "bank4", nc.vector.tensor_copy)
         flip(1, branch_sb, 0, 1, "bank5", nc.scalar.copy)
         flip(1, branch_sb, 1, 1, "bank6", nc.scalar.copy)
 
-        bias_ps = psum.tile([P, H], F32, tag="bank7")
         bias_cols = [keep.tile([P, CH_TILES], F32, name="bias_cols%d" % v) for v in range(2)]
 
         def bias_to_columns(v):
-            spot = bias_ps[:, v * CH_TILES : (v + 1) * CH_TILES]
+            bias_ps = psum.tile([P, H], F32, name="bias_ps%d" % v, tag="bank%d" % (7 - 2 * v))
+            spot = bias_ps[:, 0:CH_TILES]
             nc.tensor.matmul(out=spot, lhsT=bias_rows[v][:], rhs=pick[:, 0:CH_TILES], start=True, stop=True)
             nc.vector.tensor_copy(out=bias_cols[v][:], in_=spot)
 
@@ -238,21 +228,35 @@ def tile_bag_lstm_pb_s_kernel(
                 gate_passes(c, t)
         relu(0)
         relu(1)
-        lin_pass(0)
-        lin_pass(1)
+
+        one_minus_bag = per_row("one_minus_bag")
+        nc.vector.tensor_scalar(
+            out=one_minus_bag[:], in0=bag[:], scalar1=-1.0, scalar2=1.0, op0=ALU.mult, op1=ALU.add
+        )
+        kept = big("kept")
+
+        def keep_main(t):
+            nc.vector.tensor_scalar_mul(out=kept[t][:], in0=main_sb[:, t, :], scalar1=col(one_minus_bag, t))
+
+        keep_main(0)
         bias_to_columns(1)
+        keep_main(1)
+
+        for t in tiles:
+            gate_passes(2, t)
+        relu(2)
+        lin_pass(0)
         product(0)
-        product(1)
-        ln_cols = keep.tile([P, 2 * CH_TILES], F32)
-        ln_ps = psum.tile([P, H], F32, tag="bank7")
-        nc.tensor.matmul(out=ln_ps[:, 0 : 2 * CH_TILES], lhsT=ln_rows[:], rhs=pick[:], start=True, stop=True)
-        nc.scalar.copy(out=ln_cols[:], in_=ln_ps[:, 0 : 2 * CH_TILES])
-        for c in range(2, CH_TILES):
-            for t in tiles:
-                gate_passes(c, t)
-            relu(c)
+        for t in tiles:
+            gate_passes(3, t)
+        relu(3)
+        for c in range(1, CH_TILES):
             lin_pass(c)
             product(c)
+        ln_cols = keep.tile([P, 2 * CH_TILES], F32)
+        ln_ps = psum.tile([P, H], F32, tag="bank1")
+        nc.tensor.matmul(out=ln_ps[:, 0 : 2 * CH_TILES], lhsT=ln_rows[:], rhs=pick[:], start=True, stop=True)
+        nc.scalar.copy(out=ln_cols[:], in_=ln_ps[:, 0 : 2 * CH_TILES])
 
         h_m = [psum.tile([P, H], F32, name="h_m%d" % t, tag="bank%d" % (2 * t)) for t in tiles]
 
@@ -267,10 +271,12 @@ def tile_bag_lstm_pb_s_kernel(
                 nc.tensor.transpose(repeated[:, c * P : (c + 1) * P], column.to_broadcast([P, P]), ident[:])
             return repeated
 
-        ln_b_all = repeat_on_all_partitions(CH_TILES, "bank1")
-        for c in range(CH_TILES):
-            back_to_rows(c)
-        ln_g_all = repeat_on_all_partitions(0, "bank3")
+        back_to_rows(0)
+        back_to_rows(1)
+        ln_b_all = repeat_on_all_partitions(CH_TILES, "bank3")
+        back_to_rows(2)
+        back_to_rows(3)
+        ln_g_all = repeat_on_all_partitions(0, "bank5")
 
         ratio_sq = per_row("ratio_sq")
         ratio = per_row("ratio")

@@ -175,6 +175,10 @@ def tile_bag_lstm_pb_s_kernel(
         nc.gpsimd.tensor_scalar(
             out=eps_over_em[:], in0=inv_em[:], scalar1=BAG_EPS, scalar2=0.0, op0=ALU.mult, op1=ALU.add
         )
+        bag_unit = per_row("bag_unit")
+        nc.gpsimd.tensor_scalar(
+            out=bag_unit[:], in0=bag[:], scalar1=LN_EPS ** -0.5, scalar2=0.0, op0=ALU.mult, op1=ALU.add
+        )
         o_sb = keep.tile([P, ROW_TILES, H], BF16)
         nc.gpsimd.dma_start(out=o_sb[:], in_=by_row_tile(o))
         flip(0, main_sb, 0, ROW_TILES, "bank4", nc.vector.tensor_copy)
@@ -190,44 +194,41 @@ def tile_bag_lstm_pb_s_kernel(
             nc.vector.tensor_copy(out=bias_cols[v][:], in_=spot)
 
         spin(SPINS_BETWEEN)
-        for t in tiles:
-            quantise(0, t, 1)
-            quantise(1, t, 1)
+        quantise(0, 0, 1)
+        quantise(1, 0, 1)
         bias_to_columns(0)
+        quantise(0, 1, 1)
+        quantise(1, 1, 1)
 
         gate = [psum.tile([P, B], F32, name="gate%d" % c, tag="bank%d" % (2 * c)) for c in range(CH_TILES)]
         lin = [psum.tile([P, B], F32, name="lin%d" % c, tag="bank%d" % (2 * c + 1)) for c in range(CH_TILES)]
         open_gate = keep.tile([P, CH_TILES, B], F32)
         h_cols = keep.tile([P, CH_TILES, B], F32)
 
-        def gate_passes(c, t):
-            rows = slice(t * P, (t + 1) * P)
+        def row_cols(t):
+            return slice(t * P, (t + 1) * P)
+
+        def gate_passes(t, c):
+            rows = row_cols(t)
             mx_pass(gate[c][:, rows], 0, c, 0, rows, True, False)
             mx_pass(gate[c][:, rows], 1, c, 1, rows, False, True)
-
-        def relu(c):
             nc.scalar.activation(
-                out=open_gate[:, c, :], in_=gate[c][:], func=ACT.Relu, bias=bias_cols[0][:, c : c + 1]
+                out=open_gate[:, c, rows], in_=gate[c][:, rows], func=ACT.Relu, bias=bias_cols[0][:, c : c + 1]
             )
 
         def lin_pass(c):
             mx_pass(lin[c][:], 2, c, 1, slice(0, B), True, True)
 
-        def product(c):
+        def product(t, c):
+            rows = row_cols(t)
             nc.vector.scalar_tensor_tensor(
-                out=h_cols[:, c, :],
-                in0=lin[c][:],
+                out=h_cols[:, c, rows],
+                in0=lin[c][:, rows],
                 scalar=bias_cols[1][:, c : c + 1],
-                in1=open_gate[:, c, :],
+                in1=open_gate[:, c, rows],
                 op0=ALU.add,
                 op1=ALU.mult,
             )
-
-        for t in tiles:
-            for c in range(2):
-                gate_passes(c, t)
-        relu(0)
-        relu(1)
 
         one_minus_bag = per_row("one_minus_bag")
         nc.vector.tensor_scalar(
@@ -238,31 +239,31 @@ def tile_bag_lstm_pb_s_kernel(
         def keep_main(t):
             nc.vector.tensor_scalar_mul(out=kept[t][:], in0=main_sb[:, t, :], scalar1=col(one_minus_bag, t))
 
+        for c in range(CH_TILES):
+            gate_passes(0, c)
         keep_main(0)
         bias_to_columns(1)
         keep_main(1)
-
-        for t in tiles:
-            gate_passes(2, t)
-        relu(2)
-        lin_pass(0)
-        product(0)
-        for t in tiles:
-            gate_passes(3, t)
-        relu(3)
-        for c in range(1, CH_TILES):
+        for c in range(2):
+            gate_passes(1, c)
+        for c in range(CH_TILES):
             lin_pass(c)
-            product(c)
+            product(0, c)
         ln_cols = keep.tile([P, 2 * CH_TILES], F32)
-        ln_ps = psum.tile([P, H], F32, tag="bank1")
-        nc.tensor.matmul(out=ln_ps[:, 0 : 2 * CH_TILES], lhsT=ln_rows[:], rhs=pick[:], start=True, stop=True)
-        nc.scalar.copy(out=ln_cols[:], in_=ln_ps[:, 0 : 2 * CH_TILES])
+        ln_ps = psum.tile([P, H], F32, tag="bank0")
+        ln_spot = ln_ps[:, 0 : 2 * CH_TILES]
+        nc.tensor.matmul(out=ln_spot, lhsT=ln_rows[:], rhs=pick[:], start=True, stop=True)
+        nc.scalar.copy(out=ln_cols[:], in_=ln_spot)
+        for c in range(2, CH_TILES):
+            gate_passes(1, c)
+        for c in range(CH_TILES):
+            product(1, c)
 
-        h_m = [psum.tile([P, H], F32, name="h_m%d" % t, tag="bank%d" % (2 * t)) for t in tiles]
+        h_m = [psum.tile([P, H], F32, name="h_m%d" % t, tag="bank%d" % (4 * t)) for t in tiles]
 
-        def back_to_rows(c):
-            for t in tiles:
-                nc.tensor.transpose(h_m[t][:, c * P : (c + 1) * P], h_cols[:, c, t * P : (t + 1) * P], ident[:])
+        def back_to_rows(t):
+            for c in range(CH_TILES):
+                nc.tensor.transpose(h_m[t][:, c * P : (c + 1) * P], h_cols[:, c, row_cols(t)], ident[:])
 
         def repeat_on_all_partitions(first_col, bank):
             repeated = psum.tile([P, H], F32, name="repeated%d" % first_col, tag=bank)
@@ -271,12 +272,10 @@ def tile_bag_lstm_pb_s_kernel(
                 nc.tensor.transpose(repeated[:, c * P : (c + 1) * P], column.to_broadcast([P, P]), ident[:])
             return repeated
 
+        ln_b_all = repeat_on_all_partitions(CH_TILES, "bank2")
         back_to_rows(0)
         back_to_rows(1)
-        ln_b_all = repeat_on_all_partitions(CH_TILES, "bank3")
-        back_to_rows(2)
-        back_to_rows(3)
-        ln_g_all = repeat_on_all_partitions(0, "bank5")
+        ln_g_all = repeat_on_all_partitions(0, "bank1")
 
         ratio_sq = per_row("ratio_sq")
         ratio = per_row("ratio")
@@ -293,7 +292,7 @@ def tile_bag_lstm_pb_s_kernel(
             )
 
         stretch = per_row("stretch")
-        eps_row = per_row("eps_row")
+        stretch_sq = per_row("stretch_sq")
         pre = big("pre")
         pre_sum = per_row("pre_sum")
         mean = per_row("mean")
@@ -314,19 +313,21 @@ def tile_bag_lstm_pb_s_kernel(
                 op1=ALU.add,
                 accum_out=col(pre_sum, t),
             )
-            nc.vector.scalar_tensor_tensor(
-                out=col(eps_row, t), in0=col(stretch, t), scalar=LN_EPS, in1=col(stretch, t), op0=ALU.mult, op1=ALU.mult
-            )
+            nc.gpsimd.tensor_tensor(out=col(stretch_sq, t), in0=col(stretch, t), in1=col(stretch, t), op=ALU.mult)
+            nc.scalar.activation(out=col(mean, t), in_=col(pre_sum, t), func=ACT.Copy, scale=1.0 / H)
             nc.scalar.activation(
                 out=squares[:], in_=pre[t][:], func=ACT.Square, scale=-1.0 * H, bias=col(pre_sum, t), accum_out=col(dev_sq, t)
             )
             nc.scalar.activation(
-                out=col(spread, t), in_=col(dev_sq, t), func=ACT.Identity, scale=1.0 / H / H / H, bias=col(eps_row, t)
+                out=col(spread, t),
+                in_=col(dev_sq, t),
+                func=ACT.Identity,
+                scale=1.0 / (LN_EPS * H * H * H),
+                bias=col(stretch_sq, t),
             )
-        nc.vector.tensor_scalar_mul(out=mean[:], in0=pre_sum[:], scalar1=1.0 / H)
         for t in tiles:
             nc.gpsimd.tensor_tensor(out=col(spread, t), in0=col(spread, t), in1=col(neg_half, t), op=ALU.pow)
-            nc.gpsimd.tensor_tensor(out=col(factor, t), in0=col(spread, t), in1=col(bag, t), op=ALU.mult)
+            nc.gpsimd.tensor_tensor(out=col(factor, t), in0=col(spread, t), in1=col(bag_unit, t), op=ALU.mult)
             nc.vector.scalar_tensor_tensor(
                 out=centred[t][:], in0=pre[t][:], scalar=col(mean, t), in1=ln_g_all[:], op0=ALU.subtract, op1=ALU.mult
             )

@@ -164,8 +164,16 @@ def tile_bag_lstm_pb_s_kernel(
 
         squares = keep.tile([P, H], F32)
         em_sq = per_row("em_sq")
-        for t in tiles:
+
+        def square_main(t):
             nc.scalar.activation(out=squares[:], in_=main_sb[:, t, :], func=ACT.Square, accum_out=col(em_sq, t))
+
+        square_main(0)
+        flip(0, main_sb, 0, 1, "bank4", nc.vector.tensor_copy)
+        flip(0, main_sb, 1, 1, "bank1", nc.vector.tensor_copy)
+        flip(1, branch_sb, 0, 1, "bank5", nc.scalar.copy)
+        flip(1, branch_sb, 1, 1, "bank6", nc.scalar.copy)
+        square_main(1)
         inv_em = per_row("inv_em")
         nc.gpsimd.tensor_scalar(
             out=em_sq[:], in0=em_sq[:], scalar1=EM_FLOOR * EM_FLOOR, scalar2=None, op0=ALU.max
@@ -181,9 +189,6 @@ def tile_bag_lstm_pb_s_kernel(
         )
         o_sb = keep.tile([P, ROW_TILES, H], BF16)
         nc.gpsimd.dma_start(out=o_sb[:], in_=by_row_tile(o))
-        flip(0, main_sb, 0, ROW_TILES, "bank4", nc.vector.tensor_copy)
-        flip(1, branch_sb, 0, 1, "bank5", nc.scalar.copy)
-        flip(1, branch_sb, 1, 1, "bank6", nc.scalar.copy)
 
         bias_cols = [keep.tile([P, CH_TILES], F32, name="bias_cols%d" % v) for v in range(2)]
 

@@ -19,7 +19,7 @@ H = 512
 ROW_TILES = B // P
 CH_TILES = H // P
 WORDS = H // 2
-SPINS_BEFORE = 5
+SPINS_BEFORE = 3
 SPINS_BETWEEN = 2
 LN_EPS = 1e-5
 BAG_EPS = 1e-6
@@ -82,10 +82,9 @@ def tile_bag_lstm_pb_s_kernel(
         branch_sb = keep.tile([P, ROW_TILES, H], BF16)
         nc.sync.dma_start(out=branch_sb[:], in_=by_row_tile(branch))
 
-        bias_rows = [keep.tile([P, P], BF16, name="bias_rows%d" % v) for v in range(2)]
-        for v in range(2):
-            nc.vector.memset(bias_rows[v][:].bitcast(I32), 0)
-        nc.sync.dma_start(out=bias_rows[0][0:CH_TILES, :], in_=b_mb.rearrange("(c p) -> c p", p=P))
+        rows = [keep.tile([P, P], BF16, name="rows%d" % v) for v in range(4)]
+        nc.vector.memset(rows[0][:].bitcast(I32), 0)
+        nc.sync.dma_start(out=rows[0][0:CH_TILES, :], in_=b_mb.rearrange("(c p) -> c p", p=P))
 
         w_words = keep.tile([P, 3, 2 * H], U8, align_bytes=64)
         w_scales = keep.tile([P, 3, H], U8, align_bytes=64)
@@ -99,7 +98,10 @@ def tile_bag_lstm_pb_s_kernel(
             out=w_words[:, 0:2, :].bitcast(I32),
             in_=W_mb_words.rearrange("g p n -> p g n").bitcast(I32),
         )
-        nc.sync.dma_start(out=bias_rows[1][0:CH_TILES, :], in_=b_b.rearrange("(c p) -> c p", p=P))
+        for v in range(1, 4):
+            nc.vector.memset(rows[v][:].bitcast(I32), 0)
+        nc.sync.dma_start(out=rows[1][0:CH_TILES, :], in_=b_b.rearrange("(c p) -> c p", p=P))
+        nc.sync.dma_start(out=rows[2][0:CH_TILES, :], in_=ln_b.rearrange("(c p) -> c p", p=P))
         nc.sync.dma_start(out=w_words[:, 2, :].bitcast(I32), in_=W_b_words[0].bitcast(I32))
         for r in range(4):
             nc.sync.dma_start(
@@ -110,16 +112,13 @@ def tile_bag_lstm_pb_s_kernel(
         make_identity(nc, ident[:])
         bag = keep.tile([P, ROW_TILES], BF16)
         nc.gpsimd.dma_start(out=bag[:], in_=is_bag.rearrange("(p t) one -> p (t one)", t=ROW_TILES))
-        ln_rows = keep.tile([P, P], BF16)
-        nc.vector.memset(ln_rows[:].bitcast(I32), 0)
-        nc.gpsimd.dma_start(out=ln_rows[0:CH_TILES, :], in_=ln_g.rearrange("(c p) -> c p", p=P))
-        nc.gpsimd.dma_start(out=ln_rows[CH_TILES : 2 * CH_TILES, :], in_=ln_b.rearrange("(c p) -> c p", p=P))
+        nc.gpsimd.dma_start(out=rows[3][0:CH_TILES, :], in_=ln_g.rearrange("(c p) -> c p", p=P))
 
         warm = keep.tile([P, 1], F32)
         nc.vector.memset(warm[:], 0.0)
         nc.scalar.activation(out=warm[:], in_=warm[:], func=ACT.Tanh)
-        pick = keep.tile([P, 2 * CH_TILES], BF16)
-        nc.vector.tensor_copy(out=pick[:], in_=ident[:, 0 : 2 * CH_TILES])
+        pick = keep.tile([P, CH_TILES], BF16)
+        nc.vector.tensor_copy(out=pick[:], in_=ident[:, 0:CH_TILES])
         half = per_row("half")
         nc.gpsimd.memset(half[:], 0.5)
         neg_half = per_row("neg_half")
@@ -173,16 +172,19 @@ def tile_bag_lstm_pb_s_kernel(
         flip(0, main_sb, 1, 1, "bank1", nc.vector.tensor_copy)
         flip(1, branch_sb, 0, 1, "bank5", nc.scalar.copy)
         flip(1, branch_sb, 1, 1, "bank6", nc.scalar.copy)
-        square_main(1)
         inv_em = per_row("inv_em")
-        nc.gpsimd.tensor_scalar(
-            out=em_sq[:], in0=em_sq[:], scalar1=EM_FLOOR * EM_FLOOR, scalar2=None, op0=ALU.max
-        )
-        nc.gpsimd.tensor_tensor(out=inv_em[:], in0=em_sq[:], in1=neg_half[:], op=ALU.pow)
         eps_over_em = per_row("eps_over_em")
-        nc.gpsimd.tensor_scalar(
-            out=eps_over_em[:], in0=inv_em[:], scalar1=BAG_EPS, scalar2=0.0, op0=ALU.mult, op1=ALU.add
-        )
+
+        def invert_em(t):
+            nc.gpsimd.tensor_scalar(
+                out=col(em_sq, t), in0=col(em_sq, t), scalar1=EM_FLOOR * EM_FLOOR, scalar2=None, op0=ALU.max
+            )
+            nc.gpsimd.tensor_tensor(out=col(inv_em, t), in0=col(em_sq, t), in1=col(neg_half, t), op=ALU.pow)
+            nc.gpsimd.tensor_scalar(
+                out=col(eps_over_em, t), in0=col(inv_em, t), scalar1=BAG_EPS, scalar2=0.0, op0=ALU.mult, op1=ALU.add
+            )
+
+        invert_em(0)
         bag_unit = per_row("bag_unit")
         nc.gpsimd.tensor_scalar(
             out=bag_unit[:], in0=bag[:], scalar1=LN_EPS ** -0.5, scalar2=0.0, op0=ALU.mult, op1=ALU.add
@@ -190,18 +192,19 @@ def tile_bag_lstm_pb_s_kernel(
         o_sb = keep.tile([P, ROW_TILES, H], BF16)
         nc.gpsimd.dma_start(out=o_sb[:], in_=by_row_tile(o))
 
-        bias_cols = [keep.tile([P, CH_TILES], F32, name="bias_cols%d" % v) for v in range(2)]
+        columns = [keep.tile([P, CH_TILES], F32, name="columns%d" % v) for v in range(4)]
 
-        def bias_to_columns(v):
-            bias_ps = psum.tile([P, H], F32, name="bias_ps%d" % v, tag="bank%d" % (7 - 2 * v))
-            spot = bias_ps[:, 0:CH_TILES]
-            nc.tensor.matmul(out=spot, lhsT=bias_rows[v][:], rhs=pick[:, 0:CH_TILES], start=True, stop=True)
-            nc.vector.tensor_copy(out=bias_cols[v][:], in_=spot)
+        def to_columns(v, bank, copy_out):
+            turned = psum.tile([P, H], F32, name="turned%d" % v, tag=bank)
+            nc.tensor.matmul(
+                out=turned[:, 0:CH_TILES], lhsT=rows[v][:], rhs=pick[:], start=True, stop=True
+            )
+            copy_out(out=columns[v][:], in_=turned[:, 0:CH_TILES])
 
         spin(SPINS_BETWEEN)
         quantise(0, 0, 1)
         quantise(1, 0, 1)
-        bias_to_columns(0)
+        to_columns(0, "bank3", nc.vector.tensor_copy)
         quantise(0, 1, 1)
         quantise(1, 1, 1)
 
@@ -218,7 +221,7 @@ def tile_bag_lstm_pb_s_kernel(
             mx_pass(gate[c][:, rows], 0, c, 0, rows, True, False)
             mx_pass(gate[c][:, rows], 1, c, 1, rows, False, True)
             nc.scalar.activation(
-                out=open_gate[:, c, rows], in_=gate[c][:, rows], func=ACT.Relu, bias=bias_cols[0][:, c : c + 1]
+                out=open_gate[:, c, rows], in_=gate[c][:, rows], func=ACT.Relu, bias=columns[0][:, c : c + 1]
             )
 
         def lin_pass(c):
@@ -229,7 +232,7 @@ def tile_bag_lstm_pb_s_kernel(
             nc.vector.scalar_tensor_tensor(
                 out=h_cols[:, c, rows],
                 in0=lin[c][:, rows],
-                scalar=bias_cols[1][:, c : c + 1],
+                scalar=columns[1][:, c : c + 1],
                 in1=open_gate[:, c, rows],
                 op0=ALU.add,
                 op1=ALU.mult,
@@ -246,20 +249,18 @@ def tile_bag_lstm_pb_s_kernel(
 
         for c in range(CH_TILES):
             gate_passes(0, c)
+        to_columns(1, "bank5", nc.vector.tensor_copy)
         keep_main(0)
-        bias_to_columns(1)
-        keep_main(1)
-        for c in range(2):
+        to_columns(2, "bank7", nc.scalar.copy)
+        square_main(1)
+        invert_em(1)
+        for c in range(1):
             gate_passes(1, c)
         for c in range(CH_TILES):
             lin_pass(c)
             product(0, c)
-        ln_cols = keep.tile([P, 2 * CH_TILES], F32)
-        ln_ps = psum.tile([P, H], F32, tag="bank0")
-        ln_spot = ln_ps[:, 0 : 2 * CH_TILES]
-        nc.tensor.matmul(out=ln_spot, lhsT=ln_rows[:], rhs=pick[:], start=True, stop=True)
-        nc.scalar.copy(out=ln_cols[:], in_=ln_spot)
-        for c in range(2, CH_TILES):
+        keep_main(1)
+        for c in range(1, CH_TILES):
             gate_passes(1, c)
         for c in range(CH_TILES):
             product(1, c)
@@ -270,25 +271,29 @@ def tile_bag_lstm_pb_s_kernel(
             for c in range(CH_TILES):
                 nc.tensor.transpose(h_m[t][:, c * P : (c + 1) * P], h_cols[:, c, row_cols(t)], ident[:])
 
-        def repeat_on_all_partitions(first_col, bank):
-            repeated = psum.tile([P, H], F32, name="repeated%d" % first_col, tag=bank)
+        def repeat_on_all_partitions(v, bank):
+            repeated = psum.tile([P, H], F32, name="repeated%d" % v, tag=bank)
             for c in range(CH_TILES):
-                column = ln_cols[:, first_col + c : first_col + c + 1]
+                column = columns[v][:, c : c + 1]
                 nc.tensor.transpose(repeated[:, c * P : (c + 1) * P], column.to_broadcast([P, P]), ident[:])
             return repeated
 
-        ln_b_all = repeat_on_all_partitions(CH_TILES, "bank2")
-        back_to_rows(0)
-        back_to_rows(1)
-        ln_g_all = repeat_on_all_partitions(0, "bank1")
-
         ratio_sq = per_row("ratio_sq")
         ratio = per_row("ratio")
-        for t in tiles:
+
+        def square_h(t):
             nc.scalar.activation(
                 out=squares[:], in_=h_m[t][:], func=ACT.Square, scale=col(inv_em, t), accum_out=col(ratio_sq, t)
             )
             nc.gpsimd.tensor_tensor(out=col(ratio, t), in0=col(ratio_sq, t), in1=col(half, t), op=ALU.pow)
+
+        back_to_rows(0)
+        square_h(0)
+        ln_b_all = repeat_on_all_partitions(2, "bank2")
+        to_columns(3, "bank6", nc.scalar.copy)
+        back_to_rows(1)
+        square_h(1)
+        ln_g_all = repeat_on_all_partitions(3, "bank1")
 
         rest = big("rest")
         for t in tiles:

@@ -19,7 +19,7 @@ H = 512
 ROW_TILES = B // P
 CH_TILES = H // P
 WORDS = H // 2
-SPINS_BEFORE = 3
+SPINS_BEFORE = 4
 SPINS_BETWEEN = 2
 LN_EPS = 1e-5
 BAG_EPS = 1e-6

@@ -23,7 +23,7 @@ SPINS_BEFORE = 4
 SPINS_BETWEEN = 2
 LN_EPS = 1e-5
 BAG_EPS = 1e-6
-EM_FLOOR = 1e-12
+FLOOR = 2.0**-40
 
 FLOPS = 2 * B * (2 * H) * H + 2 * B * H * H
 
@@ -119,6 +119,8 @@ def tile_bag_lstm_pb_s_kernel(
         nc.scalar.activation(out=warm[:], in_=warm[:], func=ACT.Tanh)
         pick = keep.tile([P, CH_TILES], BF16)
         nc.vector.tensor_copy(out=pick[:], in_=ident[:, 0:CH_TILES])
+        floor = keep.tile([P, 1], F32)
+        nc.vector.memset(floor[:], FLOOR)
         half = per_row("half")
         nc.gpsimd.memset(half[:], 0.5)
         neg_half = per_row("neg_half")
@@ -165,7 +167,9 @@ def tile_bag_lstm_pb_s_kernel(
         em_sq = per_row("em_sq")
 
         def square_main(t):
-            nc.scalar.activation(out=squares[:], in_=main_sb[:, t, :], func=ACT.Square, accum_out=col(em_sq, t))
+            nc.scalar.activation(
+                out=squares[:], in_=main_sb[:, t, :], func=ACT.Square, bias=floor[:], accum_out=col(em_sq, t)
+            )
 
         square_main(0)
         flip(0, main_sb, 0, 1, "bank4", nc.vector.tensor_copy)
@@ -173,22 +177,11 @@ def tile_bag_lstm_pb_s_kernel(
         flip(1, branch_sb, 0, 1, "bank5", nc.scalar.copy)
         flip(1, branch_sb, 1, 1, "bank6", nc.scalar.copy)
         inv_em = per_row("inv_em")
-        eps_over_em = per_row("eps_over_em")
 
         def invert_em(t):
-            nc.gpsimd.tensor_scalar(
-                out=col(em_sq, t), in0=col(em_sq, t), scalar1=EM_FLOOR * EM_FLOOR, scalar2=None, op0=ALU.max
-            )
             nc.gpsimd.tensor_tensor(out=col(inv_em, t), in0=col(em_sq, t), in1=col(neg_half, t), op=ALU.pow)
-            nc.gpsimd.tensor_scalar(
-                out=col(eps_over_em, t), in0=col(inv_em, t), scalar1=BAG_EPS, scalar2=0.0, op0=ALU.mult, op1=ALU.add
-            )
 
         invert_em(0)
-        bag_unit = per_row("bag_unit")
-        nc.gpsimd.tensor_scalar(
-            out=bag_unit[:], in0=bag[:], scalar1=LN_EPS ** -0.5, scalar2=0.0, op0=ALU.mult, op1=ALU.add
-        )
         o_sb = keep.tile([P, ROW_TILES, H], BF16)
         nc.gpsimd.dma_start(out=o_sb[:], in_=by_row_tile(o))
 
@@ -250,7 +243,18 @@ def tile_bag_lstm_pb_s_kernel(
         for c in range(CH_TILES):
             gate_passes(0, c)
         to_columns(1, "bank5", nc.vector.tensor_copy)
+        inv_bag = per_row("inv_bag")
+        nc.vector.tensor_scalar(
+            out=inv_bag[:], in0=bag[:], scalar1=FLOOR, scalar2=None, op0=ALU.max
+        )
+        nc.vector.reciprocal(out=inv_bag[:], in_=inv_bag[:])
         keep_main(0)
+        root_eps = per_row("root_eps")
+        nc.vector.tensor_scalar_mul(out=root_eps[:], in0=inv_bag[:], scalar1=LN_EPS**0.5)
+        inv_bag_sq = per_row("inv_bag_sq")
+        nc.vector.scalar_tensor_tensor(
+            out=inv_bag_sq[:], in0=inv_bag[:], scalar=1.0 / (H * H * H), in1=inv_bag[:], op0=ALU.mult, op1=ALU.mult
+        )
         to_columns(2, "bank7", nc.scalar.copy)
         square_main(1)
         invert_em(1)
@@ -295,6 +299,8 @@ def tile_bag_lstm_pb_s_kernel(
         square_h(1)
         ln_g_all = repeat_on_all_partitions(3, "bank1")
 
+        eps_over_em = per_row("eps_over_em")
+        nc.vector.tensor_scalar_mul(out=eps_over_em[:], in0=inv_em[:], scalar1=BAG_EPS)
         rest = big("rest")
         for t in tiles:
             nc.vector.scalar_tensor_tensor(
@@ -302,7 +308,7 @@ def tile_bag_lstm_pb_s_kernel(
             )
 
         stretch = per_row("stretch")
-        stretch_sq = per_row("stretch_sq")
+        eps_row = per_row("eps_row")
         pre = big("pre")
         pre_sum = per_row("pre_sum")
         mean = per_row("mean")
@@ -323,7 +329,9 @@ def tile_bag_lstm_pb_s_kernel(
                 op1=ALU.add,
                 accum_out=col(pre_sum, t),
             )
-            nc.gpsimd.tensor_tensor(out=col(stretch_sq, t), in0=col(stretch, t), in1=col(stretch, t), op=ALU.mult)
+            nc.scalar.activation(
+                out=col(eps_row, t), in_=col(stretch, t), func=ACT.Square, scale=col(root_eps, t)
+            )
             nc.scalar.activation(out=col(mean, t), in_=col(pre_sum, t), func=ACT.Copy, scale=1.0 / H)
             nc.scalar.activation(
                 out=squares[:], in_=pre[t][:], func=ACT.Square, scale=-1.0 * H, bias=col(pre_sum, t), accum_out=col(dev_sq, t)
@@ -332,12 +340,11 @@ def tile_bag_lstm_pb_s_kernel(
                 out=col(spread, t),
                 in_=col(dev_sq, t),
                 func=ACT.Identity,
-                scale=1.0 / (LN_EPS * H * H * H),
-                bias=col(stretch_sq, t),
+                scale=col(inv_bag_sq, t),
+                bias=col(eps_row, t),
             )
         for t in tiles:
-            nc.gpsimd.tensor_tensor(out=col(spread, t), in0=col(spread, t), in1=col(neg_half, t), op=ALU.pow)
-            nc.gpsimd.tensor_tensor(out=col(factor, t), in0=col(spread, t), in1=col(bag_unit, t), op=ALU.mult)
+            nc.gpsimd.tensor_tensor(out=col(factor, t), in0=col(spread, t), in1=col(neg_half, t), op=ALU.pow)
             nc.vector.scalar_tensor_tensor(
                 out=centred[t][:], in0=pre[t][:], scalar=col(mean, t), in1=ln_g_all[:], op0=ALU.subtract, op1=ALU.mult
             )

@@ -108,19 +108,19 @@ def tile_bag_lstm_pb_s_kernel(
                 out=w_scales[r:P:32, 2, :].bitcast(I32), in_=W_b_scales[0, r:16:4, :].bitcast(I32)
             )
 
-        ident = keep.tile([P, P], F32)
-        make_identity(nc, ident[:])
         bag = keep.tile([P, ROW_TILES], BF16)
         nc.gpsimd.dma_start(out=bag[:], in_=is_bag.rearrange("(p t) one -> p (t one)", t=ROW_TILES))
+        ident = keep.tile([P, P], F32)
+        make_identity(nc, ident[:])
         nc.gpsimd.dma_start(out=rows[3][0:CH_TILES, :], in_=ln_g.rearrange("(c p) -> c p", p=P))
 
         warm = keep.tile([P, 1], F32)
         nc.vector.memset(warm[:], 0.0)
         nc.scalar.activation(out=warm[:], in_=warm[:], func=ACT.Tanh)
-        pick = keep.tile([P, CH_TILES], BF16)
-        nc.vector.tensor_copy(out=pick[:], in_=ident[:, 0:CH_TILES])
         floor = keep.tile([P, 1], F32)
         nc.vector.memset(floor[:], FLOOR)
+        pick = keep.tile([P, CH_TILES], BF16)
+        nc.vector.tensor_copy(out=pick[:], in_=ident[:, 0:CH_TILES])
         half = per_row("half")
         nc.gpsimd.memset(half[:], 0.5)
         neg_half = per_row("neg_half")
@@ -171,17 +171,14 @@ def tile_bag_lstm_pb_s_kernel(
                 out=squares[:], in_=main_sb[:, t, :], func=ACT.Square, bias=floor[:], accum_out=col(em_sq, t)
             )
 
-        square_main(0)
+        for t in tiles:
+            square_main(t)
         flip(0, main_sb, 0, 1, "bank4", nc.vector.tensor_copy)
         flip(0, main_sb, 1, 1, "bank1", nc.vector.tensor_copy)
         flip(1, branch_sb, 0, 1, "bank5", nc.scalar.copy)
         flip(1, branch_sb, 1, 1, "bank6", nc.scalar.copy)
         inv_em = per_row("inv_em")
-
-        def invert_em(t):
-            nc.gpsimd.tensor_tensor(out=col(inv_em, t), in0=col(em_sq, t), in1=col(neg_half, t), op=ALU.pow)
-
-        invert_em(0)
+        nc.gpsimd.tensor_tensor(out=inv_em[:], in0=em_sq[:], in1=neg_half[:], op=ALU.pow)
         o_sb = keep.tile([P, ROW_TILES, H], BF16)
         nc.gpsimd.dma_start(out=o_sb[:], in_=by_row_tile(o))
 
@@ -235,34 +232,36 @@ def tile_bag_lstm_pb_s_kernel(
         nc.vector.tensor_scalar(
             out=one_minus_bag[:], in0=bag[:], scalar1=-1.0, scalar2=1.0, op0=ALU.mult, op1=ALU.add
         )
+        inv_bag = per_row("inv_bag")
+        nc.vector.tensor_scalar(out=inv_bag[:], in0=bag[:], scalar1=FLOOR, scalar2=None, op0=ALU.max)
         kept = big("kept")
 
         def keep_main(t):
             nc.vector.tensor_scalar_mul(out=kept[t][:], in0=main_sb[:, t, :], scalar1=col(one_minus_bag, t))
 
-        for c in range(CH_TILES):
-            gate_passes(0, c)
+        gate_passes(0, 0)
         to_columns(1, "bank5", nc.vector.tensor_copy)
-        inv_bag = per_row("inv_bag")
-        nc.vector.tensor_scalar(
-            out=inv_bag[:], in0=bag[:], scalar1=FLOOR, scalar2=None, op0=ALU.max
-        )
-        nc.vector.reciprocal(out=inv_bag[:], in_=inv_bag[:])
+        for c in range(1, CH_TILES):
+            gate_passes(0, c)
         keep_main(0)
-        root_eps = per_row("root_eps")
-        nc.vector.tensor_scalar_mul(out=root_eps[:], in0=inv_bag[:], scalar1=LN_EPS**0.5)
-        inv_bag_sq = per_row("inv_bag_sq")
-        nc.vector.scalar_tensor_tensor(
-            out=inv_bag_sq[:], in0=inv_bag[:], scalar=1.0 / (H * H * H), in1=inv_bag[:], op0=ALU.mult, op1=ALU.mult
-        )
-        to_columns(2, "bank7", nc.scalar.copy)
-        square_main(1)
-        invert_em(1)
-        for c in range(1):
-            gate_passes(1, c)
-        for c in range(CH_TILES):
+        nc.vector.reciprocal(out=inv_bag[:], in_=inv_bag[:])
+        to_columns(2, "bank7", nc.vector.tensor_copy)
+        for c in range(2):
             lin_pass(c)
             product(0, c)
+        gate_passes(1, 0)
+        for c in range(2, CH_TILES):
+            lin_pass(c)
+            product(0, c)
+        inv_bag_sq = per_row("inv_bag_sq")
+        nc.vector.scalar_tensor_tensor(
+            out=inv_bag_sq[:],
+            in0=inv_bag[:],
+            scalar=1.0 / (LN_EPS * H * H * H),
+            in1=inv_bag[:],
+            op0=ALU.mult,
+            op1=ALU.mult,
+        )
         keep_main(1)
         for c in range(1, CH_TILES):
             gate_passes(1, c)
@@ -291,10 +290,13 @@ def tile_bag_lstm_pb_s_kernel(
             )
             nc.gpsimd.tensor_tensor(out=col(ratio, t), in0=col(ratio_sq, t), in1=col(half, t), op=ALU.pow)
 
+        def scaled_copy(out, in_):
+            nc.scalar.activation(out=out, in_=in_, func=ACT.Copy, scale=LN_EPS**-0.5)
+
         back_to_rows(0)
         square_h(0)
         ln_b_all = repeat_on_all_partitions(2, "bank2")
-        to_columns(3, "bank6", nc.scalar.copy)
+        to_columns(3, "bank6", scaled_copy)
         back_to_rows(1)
         square_h(1)
         ln_g_all = repeat_on_all_partitions(3, "bank1")
@@ -302,9 +304,16 @@ def tile_bag_lstm_pb_s_kernel(
         eps_over_em = per_row("eps_over_em")
         nc.vector.tensor_scalar_mul(out=eps_over_em[:], in0=inv_em[:], scalar1=BAG_EPS)
         rest = big("rest")
-        for t in tiles:
+        halves = [slice(0, H // 2), slice(H // 2, H)]
+
+        def make_rest(t, cols):
             nc.vector.scalar_tensor_tensor(
-                out=rest[t][:], in0=ln_b_all[:], scalar=col(bag, t), in1=kept[t][:], op0=ALU.mult, op1=ALU.add
+                out=rest[t][:, cols],
+                in0=ln_b_all[:, cols],
+                scalar=col(bag, t),
+                in1=kept[t][:, cols],
+                op0=ALU.mult,
+                op1=ALU.add,
             )
 
         stretch = per_row("stretch")
@@ -316,10 +325,23 @@ def tile_bag_lstm_pb_s_kernel(
         spread = per_row("spread")
         factor = per_row("factor")
         centred = big("centred")
+        def make_factor(t):
+            nc.scalar.activation(
+                out=col(spread, t), in_=col(dev_sq, t), func=ACT.Identity, scale=col(inv_bag_sq, t), bias=col(eps_row, t)
+            )
+            nc.gpsimd.tensor_tensor(out=col(factor, t), in0=col(spread, t), in1=col(neg_half, t), op=ALU.pow)
+
+        make_rest(0, slice(0, H))
         for t in tiles:
             nc.vector.tensor_scalar(
                 out=col(stretch, t), in0=col(ratio, t), scalar1=col(eps_over_em, t), scalar2=1.0, op0=ALU.add, op1=ALU.max
             )
+            nc.scalar.activation(
+                out=col(eps_row, t), in_=col(stretch, t), func=ACT.Square, scale=col(inv_bag, t)
+            )
+            if t == 1:
+                make_factor(0)
+            make_rest(1, halves[t])
             nc.vector.scalar_tensor_tensor(
                 out=pre[t][:],
                 in0=main_sb[:, t, :],
@@ -329,22 +351,12 @@ def tile_bag_lstm_pb_s_kernel(
                 op1=ALU.add,
                 accum_out=col(pre_sum, t),
             )
-            nc.scalar.activation(
-                out=col(eps_row, t), in_=col(stretch, t), func=ACT.Square, scale=col(root_eps, t)
-            )
             nc.scalar.activation(out=col(mean, t), in_=col(pre_sum, t), func=ACT.Copy, scale=1.0 / H)
             nc.scalar.activation(
                 out=squares[:], in_=pre[t][:], func=ACT.Square, scale=-1.0 * H, bias=col(pre_sum, t), accum_out=col(dev_sq, t)
             )
-            nc.scalar.activation(
-                out=col(spread, t),
-                in_=col(dev_sq, t),
-                func=ACT.Identity,
-                scale=col(inv_bag_sq, t),
-                bias=col(eps_row, t),
-            )
+        make_factor(1)
         for t in tiles:
-            nc.gpsimd.tensor_tensor(out=col(factor, t), in0=col(spread, t), in1=col(neg_half, t), op=ALU.pow)
             nc.vector.scalar_tensor_tensor(
                 out=centred[t][:], in0=pre[t][:], scalar=col(mean, t), in1=ln_g_all[:], op0=ALU.subtract, op1=ALU.mult
             )
@@ -352,7 +364,6 @@ def tile_bag_lstm_pb_s_kernel(
         shift_c = big("shift_c")
         squashed = big("squashed")
         h_out = big("h_out")
-        halves = [slice(0, H // 2), slice(H // 2, H)]
         for t in tiles:
             for half_row in halves:
                 nc.vector.scalar_tensor_tensor(

from contextlib import ExitStack

import concourse.mybir as mybir
from concourse.masks import make_identity

FP8X4 = mybir.dt.float8_e4m3fn_x4
FP4X4 = mybir.dt.float4_e2m1fn_x4
BF16 = mybir.dt.bfloat16
F32 = mybir.dt.float32
I32 = mybir.dt.int32
U32 = mybir.dt.uint32
U8 = mybir.dt.uint8
ALU = mybir.AluOpType
ACT = mybir.ActivationFunctionType

P = 128
B = 256
H = 512
ROW_TILES = B // P
CH_TILES = H // P
WORDS = H // 2
SPINS_BEFORE = 4
SPINS_BETWEEN = 2
LN_EPS = 1e-5
BAG_EPS = 1e-6
FLOOR = 2.0**-40

FLOPS = 2 * B * (2 * H) * H + 2 * B * H * H


def tile_bag_lstm_pb_s_kernel(
    tc,
    main,
    branch,
    o,
    is_bag,
    W_mb_words,
    W_mb_scales,
    b_mb,
    W_b_words,
    W_b_scales,
    b_b,
    ln_g,
    ln_b,
    out_0,
    out_1,
):
    nc = tc.nc
    tiles = range(ROW_TILES)

    def by_row_tile(ap):
        return ap.rearrange("(p t) c -> p t c", t=ROW_TILES)

    def col(per_row, t):
        return per_row[:, t : t + 1]

    with ExitStack() as ctx:
        keep = ctx.enter_context(tc.tile_pool(name="keep", bufs=1))
        psum = ctx.enter_context(tc.psum_pool(name="psum", bufs=1))
        ctx.enter_context(tc.manual_schedule())

        def big(name):
            return [keep.tile([P, H], F32, name="%s%d" % (name, t)) for t in tiles]

        def per_row(name):
            return keep.tile([P, ROW_TILES], F32, name=name)

        still = keep.tile([P, 2 * P], F32)
        nc.vector.memset(still[:], 0.0)
        spin_ps = psum.tile([P, H], F32, tag="bank3")

        def spin(times):
            for i in range(times):
                nc.tensor.matmul(
                    out=spin_ps[:, 0:P], lhsT=still[:, 0:P], rhs=still[:, P : 2 * P], start=True, stop=True
                )

        spin(SPINS_BEFORE)

        main_sb = keep.tile([P, ROW_TILES, H], BF16)
        nc.sync.dma_start(out=main_sb[:], in_=by_row_tile(main))
        branch_sb = keep.tile([P, ROW_TILES, H], BF16)
        nc.sync.dma_start(out=branch_sb[:], in_=by_row_tile(branch))

        rows = [keep.tile([P, P], BF16, name="rows%d" % v) for v in range(4)]
        nc.vector.memset(rows[0][:].bitcast(I32), 0)
        nc.sync.dma_start(out=rows[0][0:CH_TILES, :], in_=b_mb.rearrange("(c p) -> c p", p=P))

        w_words = keep.tile([P, 3, 2 * H], U8, align_bytes=64)
        w_scales = keep.tile([P, 3, H], U8, align_bytes=64)
        nc.vector.memset(w_scales[:].rearrange("p w n -> p (w n)").bitcast(I32), 0)
        for r in range(4):
            nc.sync.dma_start(
                out=w_scales[r:P:32, 0:2, :].bitcast(I32),
                in_=W_mb_scales[:, r:16:4, :].rearrange("g q n -> q g n").bitcast(I32),
            )
        nc.sync.dma_start(
            out=w_words[:, 0:2, :].bitcast(I32),
            in_=W_mb_words.rearrange("g p n -> p g n").bitcast(I32),
        )
        for v in range(1, 4):
            nc.vector.memset(rows[v][:].bitcast(I32), 0)
        nc.sync.dma_start(out=rows[1][0:CH_TILES, :], in_=b_b.rearrange("(c p) -> c p", p=P))
        nc.sync.dma_start(out=rows[2][0:CH_TILES, :], in_=ln_b.rearrange("(c p) -> c p", p=P))
        nc.sync.dma_start(out=w_words[:, 2, :].bitcast(I32), in_=W_b_words[0].bitcast(I32))
        for r in range(4):
            nc.sync.dma_start(
                out=w_scales[r:P:32, 2, :].bitcast(I32), in_=W_b_scales[0, r:16:4, :].bitcast(I32)
            )

        bag = keep.tile([P, ROW_TILES], BF16)
        nc.gpsimd.dma_start(out=bag[:], in_=is_bag.rearrange("(p t) one -> p (t one)", t=ROW_TILES))
        ident = keep.tile([P, P], F32)
        make_identity(nc, ident[:])
        nc.gpsimd.dma_start(out=rows[3][0:CH_TILES, :], in_=ln_g.rearrange("(c p) -> c p", p=P))

        warm = keep.tile([P, 1], F32)
        nc.vector.memset(warm[:], 0.0)
        nc.scalar.activation(out=warm[:], in_=warm[:], func=ACT.Tanh)
        floor = keep.tile([P, 1], F32)
        nc.vector.memset(floor[:], FLOOR)
        pick = keep.tile([P, CH_TILES], BF16)
        nc.vector.tensor_copy(out=pick[:], in_=ident[:, 0:CH_TILES])
        half = per_row("half")
        nc.gpsimd.memset(half[:], 0.5)
        neg_half = per_row("neg_half")
        nc.gpsimd.memset(neg_half[:], -0.5)

        x_codes = keep.tile([P, 2, B], U32, align_bytes=64)
        x_scales = keep.tile([P, 2, B], U8, align_bytes=64)

        grouped = [keep.tile([P, 4 * B], BF16, align_bytes=64, name="grouped%d" % g) for g in range(2)]

        def flip(g, x_sb, first, count, bank, copy_out):
            flipped = psum.tile([P, 2, count * P], F32, name="flipped%d%d" % (g, first), tag=bank)
            for i in range(count):
                words = x_sb[:, first + i, :].bitcast(F32)
                for u in range(2):
                    nc.tensor.transpose(flipped[:, u, i * P : (i + 1) * P], words[:, u:WORDS:2], ident[:])
            copy_out(
                out=grouped[g][:, 4 * first * P : 4 * (first + count) * P]
                .bitcast(F32)
                .rearrange("p (c u) -> p c u", u=2),
                in_=flipped[:].rearrange("p u c -> p c u"),
            )

        def quantise(g, first, count):
            rows = slice(first * P, (first + count) * P)
            nc.vector.quantize_mx(
                out=x_codes[:, g, rows].bitcast(FP8X4),
                scales=x_scales[:, g, rows],
                in_=grouped[g][:, 4 * first * P : 4 * (first + count) * P],
            )

        def mx_pass(out, w, c, g, cols, start, stop):
            nc.tensor.matmul_mx(
                out=out,
                lhsT=w_words[:, w, 2 * c * P : 2 * (c + 1) * P].bitcast(FP4X4),
                lhsT_scale=w_scales[:, w, c * P : (c + 1) * P],
                rhs=x_codes[:, g, cols].bitcast(FP8X4),
                rhs_scale=x_scales[:, g, cols],
                start=start,
                stop=stop,
            )

        squares = keep.tile([P, H], F32)
        em_sq = per_row("em_sq")

        def square_main(t):
            nc.scalar.activation(
                out=squares[:], in_=main_sb[:, t, :], func=ACT.Square, bias=floor[:], accum_out=col(em_sq, t)
            )

        for t in tiles:
            square_main(t)
        flip(0, main_sb, 0, 1, "bank4", nc.vector.tensor_copy)
        flip(0, main_sb, 1, 1, "bank1", nc.vector.tensor_copy)
        flip(1, branch_sb, 0, 1, "bank5", nc.scalar.copy)
        flip(1, branch_sb, 1, 1, "bank6", nc.scalar.copy)
        inv_em = per_row("inv_em")
        nc.gpsimd.tensor_tensor(out=inv_em[:], in0=em_sq[:], in1=neg_half[:], op=ALU.pow)
        o_sb = keep.tile([P, ROW_TILES, H], BF16)
        nc.gpsimd.dma_start(out=o_sb[:], in_=by_row_tile(o))

        columns = [keep.tile([P, CH_TILES], F32, name="columns%d" % v) for v in range(4)]

        def to_columns(v, bank, copy_out):
            turned = psum.tile([P, H], F32, name="turned%d" % v, tag=bank)
            nc.tensor.matmul(
                out=turned[:, 0:CH_TILES], lhsT=rows[v][:], rhs=pick[:], start=True, stop=True
            )
            copy_out(out=columns[v][:], in_=turned[:, 0:CH_TILES])

        spin(SPINS_BETWEEN)
        quantise(0, 0, 1)
        quantise(1, 0, 1)
        to_columns(0, "bank3", nc.vector.tensor_copy)
        quantise(0, 1, 1)
        quantise(1, 1, 1)

        gate = [psum.tile([P, B], F32, name="gate%d" % c, tag="bank%d" % (2 * c)) for c in range(CH_TILES)]
        lin = [psum.tile([P, B], F32, name="lin%d" % c, tag="bank%d" % (2 * c + 1)) for c in range(CH_TILES)]
        open_gate = keep.tile([P, CH_TILES, B], F32)
        h_cols = keep.tile([P, CH_TILES, B], F32)

        def row_cols(t):
            return slice(t * P, (t + 1) * P)

        def gate_passes(t, c):
            rows = row_cols(t)
            mx_pass(gate[c][:, rows], 0, c, 0, rows, True, False)
            mx_pass(gate[c][:, rows], 1, c, 1, rows, False, True)
            nc.scalar.activation(
                out=open_gate[:, c, rows], in_=gate[c][:, rows], func=ACT.Relu, bias=columns[0][:, c : c + 1]
            )

        def lin_pass(c):
            mx_pass(lin[c][:], 2, c, 1, slice(0, B), True, True)

        def product(t, c):
            rows = row_cols(t)
            nc.vector.scalar_tensor_tensor(
                out=h_cols[:, c, rows],
                in0=lin[c][:, rows],
                scalar=columns[1][:, c : c + 1],
                in1=open_gate[:, c, rows],
                op0=ALU.add,
                op1=ALU.mult,
            )

        one_minus_bag = per_row("one_minus_bag")
        nc.vector.tensor_scalar(
            out=one_minus_bag[:], in0=bag[:], scalar1=-1.0, scalar2=1.0, op0=ALU.mult, op1=ALU.add
        )
        inv_bag = per_row("inv_bag")
        nc.vector.tensor_scalar(out=inv_bag[:], in0=bag[:], scalar1=FLOOR, scalar2=None, op0=ALU.max)
        kept = big("kept")

        def keep_main(t):
            nc.vector.tensor_scalar_mul(out=kept[t][:], in0=main_sb[:, t, :], scalar1=col(one_minus_bag, t))

        gate_passes(0, 0)
        to_columns(1, "bank5", nc.vector.tensor_copy)
        for c in range(1, CH_TILES):
            gate_passes(0, c)
        keep_main(0)
        nc.vector.reciprocal(out=inv_bag[:], in_=inv_bag[:])
        to_columns(2, "bank7", nc.vector.tensor_copy)
        for c in range(2):
            lin_pass(c)
            product(0, c)
        gate_passes(1, 0)
        for c in range(2, CH_TILES):
            lin_pass(c)
            product(0, c)
        inv_bag_sq = per_row("inv_bag_sq")
        nc.vector.scalar_tensor_tensor(
            out=inv_bag_sq[:],
            in0=inv_bag[:],
            scalar=1.0 / (LN_EPS * H * H * H),
            in1=inv_bag[:],
            op0=ALU.mult,
            op1=ALU.mult,
        )
        keep_main(1)
        for c in range(1, CH_TILES):
            gate_passes(1, c)
        for c in range(CH_TILES):
            product(1, c)

        h_m = [psum.tile([P, H], F32, name="h_m%d" % t, tag="bank%d" % (4 * t)) for t in tiles]

        def back_to_rows(t):
            for c in range(CH_TILES):
                nc.tensor.transpose(h_m[t][:, c * P : (c + 1) * P], h_cols[:, c, row_cols(t)], ident[:])

        def repeat_on_all_partitions(v, bank):
            repeated = psum.tile([P, H], F32, name="repeated%d" % v, tag=bank)
            for c in range(CH_TILES):
                column = columns[v][:, c : c + 1]
                nc.tensor.transpose(repeated[:, c * P : (c + 1) * P], column.to_broadcast([P, P]), ident[:])
            return repeated

        ratio_sq = per_row("ratio_sq")
        ratio = per_row("ratio")

        def square_h(t):
            nc.scalar.activation(
                out=squares[:], in_=h_m[t][:], func=ACT.Square, scale=col(inv_em, t), accum_out=col(ratio_sq, t)
            )
            nc.gpsimd.tensor_tensor(out=col(ratio, t), in0=col(ratio_sq, t), in1=col(half, t), op=ALU.pow)

        def scaled_copy(out, in_):
            nc.scalar.activation(out=out, in_=in_, func=ACT.Copy, scale=LN_EPS**-0.5)

        back_to_rows(0)
        square_h(0)
        ln_b_all = repeat_on_all_partitions(2, "bank2")
        to_columns(3, "bank6", scaled_copy)
        back_to_rows(1)
        square_h(1)
        ln_g_all = repeat_on_all_partitions(3, "bank1")

        eps_over_em = per_row("eps_over_em")
        nc.vector.tensor_scalar_mul(out=eps_over_em[:], in0=inv_em[:], scalar1=BAG_EPS)
        rest = big("rest")
        halves = [slice(0, H // 2), slice(H // 2, H)]

        def make_rest(t, cols):
            nc.vector.scalar_tensor_tensor(
                out=rest[t][:, cols],
                in0=ln_b_all[:, cols],
                scalar=col(bag, t),
                in1=kept[t][:, cols],
                op0=ALU.mult,
                op1=ALU.add,
            )

        stretch = per_row("stretch")
        eps_row = per_row("eps_row")
        pre = big("pre")
        pre_sum = per_row("pre_sum")
        mean = per_row("mean")
        dev_sq = per_row("dev_sq")
        spread = per_row("spread")
        factor = per_row("factor")
        centred = big("centred")
        def make_factor(t):
            nc.scalar.activation(
                out=col(spread, t), in_=col(dev_sq, t), func=ACT.Identity, scale=col(inv_bag_sq, t), bias=col(eps_row, t)
            )
            nc.gpsimd.tensor_tensor(out=col(factor, t), in0=col(spread, t), in1=col(neg_half, t), op=ALU.pow)

        make_rest(0, slice(0, H))
        for t in tiles:
            nc.vector.tensor_scalar(
                out=col(stretch, t), in0=col(ratio, t), scalar1=col(eps_over_em, t), scalar2=1.0, op0=ALU.add, op1=ALU.max
            )
            nc.scalar.activation(
                out=col(eps_row, t), in_=col(stretch, t), func=ACT.Square, scale=col(inv_bag, t)
            )
            if t == 1:
                make_factor(0)
            make_rest(1, halves[t])
            nc.vector.scalar_tensor_tensor(
                out=pre[t][:],
                in0=main_sb[:, t, :],
                scalar=col(stretch, t),
                in1=h_m[t][:],
                op0=ALU.mult,
                op1=ALU.add,
                accum_out=col(pre_sum, t),
            )
            nc.scalar.activation(out=col(mean, t), in_=col(pre_sum, t), func=ACT.Copy, scale=1.0 / H)
            nc.scalar.activation(
                out=squares[:], in_=pre[t][:], func=ACT.Square, scale=-1.0 * H, bias=col(pre_sum, t), accum_out=col(dev_sq, t)
            )
        make_factor(1)
        for t in tiles:
            nc.vector.scalar_tensor_tensor(
                out=centred[t][:], in0=pre[t][:], scalar=col(mean, t), in1=ln_g_all[:], op0=ALU.subtract, op1=ALU.mult
            )

        shift_c = big("shift_c")
        squashed = big("squashed")
        h_out = big("h_out")
        for t in tiles:
            for half_row in halves:
                nc.vector.scalar_tensor_tensor(
                    out=shift_c[t][:, half_row],
                    in0=centred[t][:, half_row],
                    scalar=col(factor, t),
                    in1=rest[t][:, half_row],
                    op0=ALU.mult,
                    op1=ALU.add,
                )
                nc.sync.dma_start(out=by_row_tile(out_1)[:, t, half_row], in_=shift_c[t][:, half_row])
                nc.scalar.activation(out=squashed[t][:, half_row], in_=shift_c[t][:, half_row], func=ACT.Tanh)
        for t in tiles:
            for half_row in halves:
                nc.vector.tensor_tensor(
                    out=h_out[t][:, half_row], in0=squashed[t][:, half_row], in1=o_sb[:, t, half_row], op=ALU.mult
                )
                nc.sync.dma_start(out=by_row_tile(out_0)[:, t, half_row], in_=h_out[t][:, half_row])
